import numpy as np
import ml_dtypes


def mxq(x, axis, fmt="e4m3"):
    dtype, down = {"e4m3": (ml_dtypes.float8_e4m3fn, 7), "e5m2": (ml_dtypes.float8_e5m2, 14)}[fmt]
    v = np.moveaxis(np.asarray(x, np.float32).astype(ml_dtypes.bfloat16).astype(np.float64), axis, -1)
    blocks = v.reshape(v.shape[:-1] + (-1, 32))
    amax = np.abs(blocks).max(-1, keepdims=True)
    byte = np.maximum(np.where(amax > 0, np.frexp(amax)[1] - 1 + 127, 0) - down, 1)
    scale = np.exp2(byte - 127.0)
    codes = (blocks / scale).astype(np.float32).astype(dtype).astype(np.float64)
    return np.moveaxis((codes * scale).reshape(v.shape), -1, axis)


WIDE = False


def mx_kscale(k):
    if not WIDE:
        return np.ones(k)
    levels = np.array([20, -20, 10, -10, 0])
    a = np.random.permutation(np.resize(levels, k // 512 * 4)).reshape(k // 512, 4)
    idx = np.arange(k)
    return np.exp2(a[idx // 512, idx % 128 // 32])


BF16 = ml_dtypes.bfloat16


def bf(x):
    return np.asarray(x, np.float32).astype(BF16)


def f64(x):
    return np.asarray(x).astype(np.float64)


Z, N, K = 4096, 32, 1024
DENSITY = 0.02
LEAK = 0.05


def setup_inputs():
    s = mx_kscale(K)
    features = np.random.standard_normal((Z, N))
    vals = np.random.standard_normal((K, N * N))
    mask = np.random.random((K, N * N)) < DENSITY
    sc = 1.0 / (N * np.sqrt(DENSITY + (1.0 - DENSITY) * LEAK**2))
    mixing_matrix = vals * np.where(mask, 1.0, LEAK) * sc / s[:, None]
    g = np.random.standard_normal((Z, K)) * np.exp2(np.random.randint(-12, 1, (Z, 1))) * s[None, :]
    return {"features": bf(features), "mixing_matrix": bf(mixing_matrix), "grad_out": bf(g)}


def reference(features, mixing_matrix, grad_out):
    f = f64(features)
    z, n = f.shape
    gouter = mxq(f64(grad_out), 1, "e5m2") @ mxq(f64(mixing_matrix), 0, "e4m3")
    gouter = gouter.reshape(z, n, n)
    return np.einsum("zij,zj->zi", gouter, f) + np.einsum("zij,zi->zj", gouter, f)

@@ -1,0 +1,193 @@
+from contextlib import ExitStack
+
+import concourse.bass as bass
+import concourse.mybir as mybir
+import concourse.tile as tile
+from concourse.masks import make_identity
+
+F32 = mybir.dt.float32
+BF16 = mybir.dt.bfloat16
+U32 = mybir.dt.uint32
+U8 = mybir.dt.uint8
+E4X4 = mybir.dt.float8_e4m3fn_x4
+E5X4 = mybir.dt.float8_e5m2_x4
+MULT = mybir.AluOpType.mult
+ADD = mybir.AluOpType.add
+AX = mybir.AxisListType.X
+
+P = 128
+Z, N, K = 4096, 32, 1024
+GROUPS = 8
+U = 4
+FLOPS = 2 * Z * K * N * N + 4 * Z * N * N
+
+
+def tile_tensorsquare_t_kernel(tc, features, mixing_matrix, grad_out, out):
+    nc = tc.nc
+    with ExitStack() as ctx:
+        keep = ctx.enter_context(tc.tile_pool(name="keep", bufs=1))
+        mprep = ctx.enter_context(tc.tile_pool(name="mprep", bufs=1))
+        graw_pool = ctx.enter_context(tc.tile_pool(name="graw", bufs=3))
+        ggr_pool = ctx.enter_context(tc.tile_pool(name="ggr", bufs=2))
+        gq_pool = ctx.enter_context(tc.tile_pool(name="gq", bufs=3))
+        fper_pool = ctx.enter_context(tc.tile_pool(name="fperp", bufs=2))
+        dsb_pool = ctx.enter_context(tc.tile_pool(name="dsbp", bufs=2))
+        ps_xt = ctx.enter_context(tc.psum_pool(name="psxt", bufs=2))
+        ps_h = ctx.enter_context(tc.psum_pool(name="psh", bufs=3))
+        ps_d = ctx.enter_context(tc.psum_pool(name="psd", bufs=1))
+        ps_dt = ctx.enter_context(tc.psum_pool(name="psdt", bufs=1))
+
+        ident = keep.tile([P, P], F32, name="ident")
+        make_identity(nc, ident[:])
+        pbufs = [keep.tile([P, U, 33 * N], F32, name="pbuf%d" % i) for i in range(2)]
+        for pb in pbufs:
+            nc.vector.memset(pb[:, :, 512:1024], 0.0)
+        f_sb = keep.tile([P, GROUPS, U, N], BF16, name="f_sb")
+        o_sb = keep.tile([P, GROUPS, U, N], F32, name="o_sb")
+        mcodes = keep.tile([P, 4, 512], U32, name="mcodes", align_bytes=64)
+        mscales = keep.tile([P, 4, 512], U8, name="mscales", align_bytes=64)
+        dcodes = keep.tile([P, 2, P], U32, name="dcodes", align_bytes=64)
+        dscales = keep.tile([P, 2, P], U8, name="dscales", align_bytes=64)
+
+        g_view = grad_out.rearrange("(g p u) k -> g p (u k)", g=GROUPS, p=P, u=U)
+        o_view = out.rearrange("(g p u) c -> g p (u c)", g=GROUPS, p=P, u=U)
+        m_view = mixing_matrix.rearrange("(g w q e) c -> g w q e c", g=2, w=2, q=P, e=2)
+
+        nc.sync.dma_start(
+            out=f_sb[:].rearrange("p g u j -> p g (u j)"),
+            in_=features.rearrange("(g p u) j -> p g (u j)", g=GROUPS, p=P, u=U),
+        )
+
+        graws = {}
+
+        def load_group(grp):
+            graw = graw_pool.tile([P, U, K], BF16, name="graw")
+            nc.sync.dma_start(out=graw[:].rearrange("p u k -> p (u k)"), in_=g_view[grp])
+            graws[grp] = graw
+
+        load_group(0)
+
+        mraw = mprep.tile([P, 2, 4, 1536], BF16, name="mraw")
+        for g in range(2):
+            for w in range(2):
+                nc.sync.dma_start(out=mraw[:, g, 2 * w : 2 * w + 2, 0:1024], in_=m_view[g, w])
+        for g in range(2):
+            for w in range(2):
+                nc.sync.dma_start(out=mraw[:, g, 2 * w : 2 * w + 2, 1024:1536], in_=m_view[g, w][:, :, 0:512])
+        load_group(1)
+
+        msw = mprep.tile([P, 2, 4, 544], BF16, name="msw")
+        mgr = mprep.tile([P, 4, 512 * 4], BF16, name="mgr", align_bytes=64)
+        mgd = mprep.tile([P, 2, P * 4], BF16, name="mgd", align_bytes=64)
+        nc.gpsimd.memset(mgd[:], 0.0)
+        for g in range(2):
+            rows_hi = mraw[:, g, :, 512:1024].rearrange("q t (a h x) -> q t a h x", h=2, x=16)
+            sw = msw[:, g, :, 0:512].rearrange("q t (a h x) -> q t a h x", h=2, x=16)
+            nc.vector.tensor_copy(out=sw[:, :, :, 0, :], in_=rows_hi[:, :, :, 1, :])
+            nc.vector.tensor_copy(out=sw[:, :, :, 1, :], in_=rows_hi[:, :, :, 0, :])
+        for g in range(2):
+            dst = mgr[:, g, :].rearrange("q (d a t) -> q d a t", a=N, t=4)
+            src_lo = mraw[:, g, :, 1 : 1 + 33 * 16].rearrange("q t (a w) -> q w a t", w=33)
+            nc.vector.tensor_copy(out=dst[:, :, 0:16, :], in_=src_lo[:, 0:16, :, :])
+            src_hi = msw[:, g, :, 1 : 1 + 33 * 16].rearrange("q t (a w) -> q w a t", w=33)
+            nc.vector.tensor_copy(out=dst[:, :, 16:32, :], in_=src_hi[:, 0:16, :, :])
+            dst2 = mgr[:, 2 + g, :].rearrange("q (d a t) -> q d a t", a=N, t=4)
+            for d in range(1, 17):
+                nc.scalar.copy(
+                    out=dst2[:, d - 1, :, :],
+                    in_=mraw[:, g, :, 32 * d : 32 * d + 33 * 31 + 1 : 33].rearrange("q t a -> q a t"),
+                )
+            nc.vector.tensor_copy(
+                out=mgd[:, g, 0 : N * 4].rearrange("q (a t) -> q a t", t=4),
+                in_=mraw[:, g, :, 0 : 33 * 31 + 1 : 33].rearrange("q t a -> q a t"),
+            )
+        for s in range(4):
+            nc.vector.quantize_mx(out=mcodes[:, s, :].bitcast(E4X4), scales=mscales[:, s, :], in_=mgr[:, s, :])
+        nc.vector.quantize_mx(
+            out=dcodes[:].rearrange("q g s -> q (g s)").bitcast(E4X4),
+            scales=dscales[:].rearrange("q g s -> q (g s)"),
+            in_=mgd[:].rearrange("q g s -> q (g s)"),
+        )
+
+        for grp in range(GROUPS):
+            if grp + 2 < GROUPS:
+                load_group(grp + 2)
+            graw = graws[grp]
+            ggr = ggr_pool.tile([P, 2 * U * P * 4], BF16, name="ggr", align_bytes=64)
+            ggr_w = ggr[:].bitcast(F32).rearrange("q (g u z w) -> q g u z w", g=2, u=U, z=P, w=2)
+            for u in range(U):
+                xt = ps_xt.tile([P, 4, P], F32, name="xt")
+                words = graw[:, u, :].bitcast(F32)
+                for b in range(4):
+                    nc.tensor.transpose(xt[:, b, :], words[:, b * P : (b + 1) * P], ident[:])
+                nc.scalar.copy(out=ggr_w[:, :, u, :, :], in_=xt[:].rearrange("q (g w) z -> q g z w", w=2))
+            gcodes = gq_pool.tile([P, 2, 512], U32, name="gcodes", align_bytes=64)
+            gscales = gq_pool.tile([P, 2, 512], U8, name="gscales", align_bytes=64)
+            for g in range(2):
+                nc.vector.quantize_mx(
+                    out=gcodes[:, g, :].bitcast(E5X4),
+                    scales=gscales[:, g, :],
+                    in_=ggr[:, g * 2048 : (g + 1) * 2048],
+                )
+            fper = fper_pool.tile([P, U, 17 * N], BF16, name="fper")
+            nc.scalar.copy(
+                out=fper[:].rearrange("p u (r j) -> p u r j", j=N),
+                in_=f_sb[:, grp, :, :].unsqueeze(2).to_broadcast([P, U, 17, N]),
+            )
+            pb = pbufs[grp % 2]
+            accd = ps_d.tile([P, 512], F32, name="accd")
+            for g in range(2):
+                nc.tensor.matmul_mx(
+                    out=accd[:],
+                    lhsT=dcodes[:, g, :].bitcast(E4X4),
+                    lhsT_scale=dscales[:, g, :],
+                    rhs=gcodes[:, g, :].bitcast(E5X4),
+                    rhs_scale=gscales[:, g, :],
+                    start=(g == 0),
+                    stop=(g == 1),
+                )
+            dsb = dsb_pool.tile([P, 512], F32, name="dsb")
+            nc.scalar.copy(out=dsb[:], in_=accd[:])
+            dtp = ps_dt.tile([P, U, P], F32, name="dtp")
+            for u in range(U):
+                nc.tensor.transpose(dtp[:, u, :], dsb[:, u * P : (u + 1) * P], ident[:])
+            nc.vector.scalar_tensor_tensor(
+                out=pb[:, :, 1024:1056],
+                in0=dtp[:, :, 0:N],
+                scalar=2.0,
+                in1=f_sb[:, grp, :, :],
+                op0=MULT,
+                op1=MULT,
+            )
+            for u in range(U):
+                h = ps_h.tile([P, 512], F32, name="h")
+                cols = slice(u * P, (u + 1) * P)
+                for i, (g, s) in enumerate(((0, 0), (0, 2), (1, 1), (1, 3))):
+                    nc.tensor.matmul_mx(
+                        out=h[:],
+                        lhsT=gcodes[:, g, cols].bitcast(E5X4),
+                        lhsT_scale=gscales[:, g, cols],
+                        rhs=mcodes[:, s, :].bitcast(E4X4),
+                        rhs_scale=mscales[:, s, :],
+                        start=(i == 0),
+                        stop=(i == 3),
+                    )
+                nc.vector.tensor_tensor(
+                    out=pb[:, u, 0:512].rearrange("p (d a) -> p d a", a=N),
+                    in0=h[:].rearrange("p (d a) -> p d a", a=N),
+                    in1=fper[:, u, 1 : 1 + 33 * 16].rearrange("p (d w) -> p d w", w=33)[:, :, 0:N],
+                    op=MULT,
+                )
+                nc.vector.tensor_tensor(
+                    out=pb[:, u, 513 : 513 + 33 * 15].rearrange("p (d w) -> p d w", w=33)[:, :, 0:N],
+                    in0=h[:, 0:480].rearrange("p (d a) -> p d a", a=N),
+                    in1=f_sb[:, grp, u, :].unsqueeze(1).to_broadcast([P, 15, N]),
+                    op=MULT,
+                )
+            nc.vector.tensor_reduce(
+                out=o_sb[:, grp, :, :],
+                in_=pb[:].rearrange("p u (r c) -> p u c r", c=N),
+                axis=AX,
+                op=ADD,
+            )
+            nc.sync.dma_start(out=o_view[grp], in_=o_sb[:, grp, :, :].rearrange("p u c -> p (u c)"))

@@ -1,8 +1,6 @@
 from contextlib import ExitStack
 
-import concourse.bass as bass
 import concourse.mybir as mybir
-import concourse.tile as tile
 from concourse.masks import make_identity
 
 F32 = mybir.dt.float32
@@ -13,13 +11,13 @@ E4X4 = mybir.dt.float8_e4m3fn_x4
 E5X4 = mybir.dt.float8_e5m2_x4
 MULT = mybir.AluOpType.mult
 ADD = mybir.AluOpType.add
-AX = mybir.AxisListType.X
 
 P = 128
 Z, N, K = 4096, 32, 1024
 GROUPS = 8
 U = 4
 FLOPS = 2 * Z * K * N * N + 4 * Z * N * N
+MANUAL = True
 
 
 def tile_tensorsquare_t_kernel(tc, features, mixing_matrix, grad_out, out):
@@ -30,16 +28,18 @@ def tile_tensorsquare_t_kernel(tc, features, mixing_matrix, grad_out, out):
         graw_pool = ctx.enter_context(tc.tile_pool(name="graw", bufs=3))
         ggr_pool = ctx.enter_context(tc.tile_pool(name="ggr", bufs=2))
         gq_pool = ctx.enter_context(tc.tile_pool(name="gq", bufs=3))
-        fper_pool = ctx.enter_context(tc.tile_pool(name="fperp", bufs=2))
-        dsb_pool = ctx.enter_context(tc.tile_pool(name="dsbp", bufs=2))
-        ps_xt = ctx.enter_context(tc.psum_pool(name="psxt", bufs=2))
+        fper_pool = ctx.enter_context(tc.tile_pool(name="fperp", bufs=3))
+        small = ctx.enter_context(tc.tile_pool(name="small", bufs=2))
+        ps_xt = ctx.enter_context(tc.psum_pool(name="psxt", bufs=3))
         ps_h = ctx.enter_context(tc.psum_pool(name="psh", bufs=3))
         ps_d = ctx.enter_context(tc.psum_pool(name="psd", bufs=1))
         ps_dt = ctx.enter_context(tc.psum_pool(name="psdt", bufs=1))
+        if MANUAL:
+            ctx.enter_context(tc.manual_schedule())
 
         ident = keep.tile([P, P], F32, name="ident")
         make_identity(nc, ident[:])
-        pbufs = [keep.tile([P, U, 33 * N], F32, name="pbuf%d" % i) for i in range(2)]
+        pbufs = [keep.tile([P, U, 1024], F32, name="pbuf%d" % i) for i in range(2)]
         for pb in pbufs:
             nc.vector.memset(pb[:, :, 512:1024], 0.0)
         f_sb = keep.tile([P, GROUPS, U, N], BF16, name="f_sb")
@@ -53,88 +53,102 @@ def tile_tensorsquare_t_kernel(tc, features, mixing_matrix, grad_out, out):
         o_view = out.rearrange("(g p u) c -> g p (u c)", g=GROUPS, p=P, u=U)
         m_view = mixing_matrix.rearrange("(g w q e) c -> g w q e c", g=2, w=2, q=P, e=2)
 
-        nc.sync.dma_start(
-            out=f_sb[:].rearrange("p g u j -> p g (u j)"),
-            in_=features.rearrange("(g p u) j -> p g (u j)", g=GROUPS, p=P, u=U),
-        )
+        graws, ggrs, gqs, fpers, dsbs, dtps, dgs, s1s, s2s, hs = {}, {}, {}, {}, {}, {}, {}, {}, {}, {}
 
-        graws = {}
-
-        def load_group(grp):
+        def load_group(n):
             graw = graw_pool.tile([P, U, K], BF16, name="graw")
-            nc.sync.dma_start(out=graw[:].rearrange("p u k -> p (u k)"), in_=g_view[grp])
-            graws[grp] = graw
-
-        load_group(0)
+            nc.sync.dma_start(out=graw[:].rearrange("p u k -> p (u k)"), in_=g_view[n])
+            graws[n] = graw
 
         mraw = mprep.tile([P, 2, 4, 1536], BF16, name="mraw")
         for g in range(2):
             for w in range(2):
                 nc.sync.dma_start(out=mraw[:, g, 2 * w : 2 * w + 2, 0:1024], in_=m_view[g, w])
-        for g in range(2):
-            for w in range(2):
-                nc.sync.dma_start(out=mraw[:, g, 2 * w : 2 * w + 2, 1024:1536], in_=m_view[g, w][:, :, 0:512])
+        load_group(0)
+        nc.sync.dma_start(
+            out=f_sb[:].rearrange("p g u j -> p g (u j)"),
+            in_=features.rearrange("(g p u) j -> p g (u j)", g=GROUPS, p=P, u=U),
+        )
         load_group(1)
+        load_group(2)
 
         msw = mprep.tile([P, 2, 4, 544], BF16, name="msw")
         mgr = mprep.tile([P, 4, 512 * 4], BF16, name="mgr", align_bytes=64)
         mgd = mprep.tile([P, 2, P * 4], BF16, name="mgd", align_bytes=64)
         nc.gpsimd.memset(mgd[:], 0.0)
         for g in range(2):
-            rows_hi = mraw[:, g, :, 512:1024].rearrange("q t (a h x) -> q t a h x", h=2, x=16)
-            sw = msw[:, g, :, 0:512].rearrange("q t (a h x) -> q t a h x", h=2, x=16)
-            nc.vector.tensor_copy(out=sw[:, :, :, 0, :], in_=rows_hi[:, :, :, 1, :])
-            nc.vector.tensor_copy(out=sw[:, :, :, 1, :], in_=rows_hi[:, :, :, 0, :])
-        for g in range(2):
-            dst = mgr[:, g, :].rearrange("q (d a t) -> q d a t", a=N, t=4)
-            src_lo = mraw[:, g, :, 1 : 1 + 33 * 16].rearrange("q t (a w) -> q w a t", w=33)
-            nc.vector.tensor_copy(out=dst[:, :, 0:16, :], in_=src_lo[:, 0:16, :, :])
-            src_hi = msw[:, g, :, 1 : 1 + 33 * 16].rearrange("q t (a w) -> q w a t", w=33)
-            nc.vector.tensor_copy(out=dst[:, :, 16:32, :], in_=src_hi[:, 0:16, :, :])
+            nc.vector.tensor_copy(out=mraw[:, g, :, 1024:1536], in_=mraw[:, g, :, 0:512])
             dst2 = mgr[:, 2 + g, :].rearrange("q (d a t) -> q d a t", a=N, t=4)
             for d in range(1, 17):
                 nc.scalar.copy(
                     out=dst2[:, d - 1, :, :],
                     in_=mraw[:, g, :, 32 * d : 32 * d + 33 * 31 + 1 : 33].rearrange("q t a -> q a t"),
                 )
+            rows_hi = mraw[:, g, :, 512:1024].rearrange("q t (a h x) -> q t a h x", h=2, x=16)
+            sw = msw[:, g, :, 0:512].rearrange("q t (a h x) -> q t a h x", h=2, x=16)
+            nc.vector.tensor_copy(out=sw[:, :, :, 0, :], in_=rows_hi[:, :, :, 1, :])
+            nc.vector.tensor_copy(out=sw[:, :, :, 1, :], in_=rows_hi[:, :, :, 0, :])
+            dst = mgr[:, g, :].rearrange("q (d a t) -> q d a t", a=N, t=4)
+            src_lo = mraw[:, g, :, 1 : 1 + 33 * 16].rearrange("q t (a w) -> q w a t", w=33)
+            nc.vector.tensor_copy(out=dst[:, :, 0:16, :], in_=src_lo[:, 0:16, :, :])
+            src_hi = msw[:, g, :, 1 : 1 + 33 * 16].rearrange("q t (a w) -> q w a t", w=33)
+            nc.vector.tensor_copy(out=dst[:, :, 16:32, :], in_=src_hi[:, 0:16, :, :])
             nc.vector.tensor_copy(
                 out=mgd[:, g, 0 : N * 4].rearrange("q (a t) -> q a t", t=4),
                 in_=mraw[:, g, :, 0 : 33 * 31 + 1 : 33].rearrange("q t a -> q a t"),
             )
-        for s in range(4):
-            nc.vector.quantize_mx(out=mcodes[:, s, :].bitcast(E4X4), scales=mscales[:, s, :], in_=mgr[:, s, :])
+            nc.vector.quantize_mx(out=mcodes[:, g, :].bitcast(E4X4), scales=mscales[:, g, :], in_=mgr[:, g, :])
+        nc.vector.quantize_mx(out=mcodes[:, 2, :].bitcast(E4X4), scales=mscales[:, 2, :], in_=mgr[:, 2, :])
         nc.vector.quantize_mx(
             out=dcodes[:].rearrange("q g s -> q (g s)").bitcast(E4X4),
             scales=dscales[:].rearrange("q g s -> q (g s)"),
             in_=mgd[:].rearrange("q g s -> q (g s)"),
         )
+        nc.vector.quantize_mx(out=mcodes[:, 3, :].bitcast(E4X4), scales=mscales[:, 3, :], in_=mgr[:, 3, :])
 
-        for grp in range(GROUPS):
-            if grp + 2 < GROUPS:
-                load_group(grp + 2)
-            graw = graws[grp]
+        def transposes(n):
             ggr = ggr_pool.tile([P, 2 * U * P * 4], BF16, name="ggr", align_bytes=64)
+            ggrs[n] = ggr
             ggr_w = ggr[:].bitcast(F32).rearrange("q (g u z w) -> q g u z w", g=2, u=U, z=P, w=2)
             for u in range(U):
                 xt = ps_xt.tile([P, 4, P], F32, name="xt")
-                words = graw[:, u, :].bitcast(F32)
+                words = graws[n][:, u, :].bitcast(F32)
                 for b in range(4):
                     nc.tensor.transpose(xt[:, b, :], words[:, b * P : (b + 1) * P], ident[:])
                 nc.scalar.copy(out=ggr_w[:, :, u, :, :], in_=xt[:].rearrange("q (g w) z -> q g z w", w=2))
+            fper = fper_pool.tile([P, U, 17 * N], BF16, name="fper")
+            fpers[n] = fper
+            nc.scalar.copy(
+                out=fper[:].rearrange("p u (r j) -> p u r j", j=N),
+                in_=f_sb[:, n, :, :].unsqueeze(2).to_broadcast([P, U, 17, N]),
+            )
+
+        def new_codes(n):
             gcodes = gq_pool.tile([P, 2, 512], U32, name="gcodes", align_bytes=64)
             gscales = gq_pool.tile([P, 2, 512], U8, name="gscales", align_bytes=64)
+            gqs[n] = (gcodes, gscales)
+
+        def quantise_tile(n, u):
+            gcodes, gscales = gqs[n]
+            for g in range(2):
+                nc.vector.quantize_mx(
+                    out=gcodes[:, g, u * P : (u + 1) * P].bitcast(E5X4),
+                    scales=gscales[:, g, u * P : (u + 1) * P],
+                    in_=ggrs[n][:, g * 2048 + u * 512 : g * 2048 + (u + 1) * 512],
+                )
+
+        def quantise(n):
+            new_codes(n)
+            gcodes, gscales = gqs[n]
             for g in range(2):
                 nc.vector.quantize_mx(
                     out=gcodes[:, g, :].bitcast(E5X4),
                     scales=gscales[:, g, :],
-                    in_=ggr[:, g * 2048 : (g + 1) * 2048],
+                    in_=ggrs[n][:, g * 2048 : (g + 1) * 2048],
                 )
-            fper = fper_pool.tile([P, U, 17 * N], BF16, name="fper")
-            nc.scalar.copy(
-                out=fper[:].rearrange("p u (r j) -> p u r j", j=N),
-                in_=f_sb[:, grp, :, :].unsqueeze(2).to_broadcast([P, U, 17, N]),
-            )
-            pb = pbufs[grp % 2]
+
+        def diag_passes(n):
+            gcodes, gscales = gqs[n]
             accd = ps_d.tile([P, 512], F32, name="accd")
             for g in range(2):
                 nc.tensor.matmul_mx(
@@ -146,48 +160,132 @@ def tile_tensorsquare_t_kernel(tc, features, mixing_matrix, grad_out, out):
                     start=(g == 0),
                     stop=(g == 1),
                 )
-            dsb = dsb_pool.tile([P, 512], F32, name="dsb")
+            dsb = small.tile([P, 512], F32, name="dsb")
+            dsbs[n] = dsb
             nc.scalar.copy(out=dsb[:], in_=accd[:])
+
+        def diag_transposes(n):
             dtp = ps_dt.tile([P, U, P], F32, name="dtp")
+            dtps[n] = dtp
             for u in range(U):
-                nc.tensor.transpose(dtp[:, u, :], dsb[:, u * P : (u + 1) * P], ident[:])
+                nc.tensor.transpose(dtp[:, u, :], dsbs[n][:, u * P : (u + 1) * P], ident[:])
+
+        def diag_product(n):
+            dg = small.tile([P, U, N], F32, name="dg")
+            dgs[n] = dg
             nc.vector.scalar_tensor_tensor(
-                out=pb[:, :, 1024:1056],
-                in0=dtp[:, :, 0:N],
-                scalar=2.0,
-                in1=f_sb[:, grp, :, :],
-                op0=MULT,
-                op1=MULT,
+                out=dg[:], in0=dtps[n][:, :, 0:N], scalar=2.0, in1=f_sb[:, n, :, :], op0=MULT, op1=MULT
             )
+
+        def passes(n, u):
+            gcodes, gscales = gqs[n]
+            h = ps_h.tile([P, 512], F32, name="h")
+            hs[(n, u)] = h
+            cols = slice(u * P, (u + 1) * P)
+            for i, (g, s) in enumerate(((0, 0), (0, 2), (1, 1), (1, 3))):
+                nc.tensor.matmul_mx(
+                    out=h[:],
+                    lhsT=gcodes[:, g, cols].bitcast(E5X4),
+                    lhsT_scale=gscales[:, g, cols],
+                    rhs=mcodes[:, s, :].bitcast(E4X4),
+                    rhs_scale=mscales[:, s, :],
+                    start=(i == 0),
+                    stop=(i == 3),
+                )
+
+        def products(n, u):
+            pb = pbufs[n % 2]
+            h = hs[(n, u)]
+            nc.vector.tensor_tensor(
+                out=pb[:, u, 0:512].rearrange("p (d a) -> p d a", a=N),
+                in0=h[:].rearrange("p (d a) -> p d a", a=N),
+                in1=fpers[n][:, u, 1 : 1 + 33 * 16].rearrange("p (d w) -> p d w", w=33)[:, :, 0:N],
+                op=MULT,
+            )
+            nc.vector.tensor_tensor(
+                out=pb[:, u, 513 : 513 + 33 * 15].rearrange("p (d w) -> p d w", w=33)[:, :, 0:N],
+                in0=h[:, 0:480].rearrange("p (d a) -> p d a", a=N),
+                in1=f_sb[:, n, u, :].unsqueeze(1).to_broadcast([P, 15, N]),
+                op=MULT,
+            )
+
+        def pool_add1(n, half):
+            if half == 0:
+                s1 = small.tile([P, U, 512], F32, name="s1")
+                s1s[n] = s1
+            us = slice(2 * half, 2 * half + 2)
+            pb = pbufs[n % 2]
+            nc.gpsimd.tensor_tensor(out=s1s[n][:, us, :], in0=pb[:, us, 0:512], in1=pb[:, us, 512:1024], op=ADD)
+
+        def pool_add2(n, us):
+            if n not in s2s:
+                s2 = small.tile([P, U, 256], F32, name="s2")
+                s2s[n] = s2
+            nc.gpsimd.tensor_tensor(out=s2s[n][:, us, :], in0=s1s[n][:, us, 0:256], in1=s1s[n][:, us, 256:512], op=ADD)
+
+        def vector_adds(n, us):
+            pb = pbufs[n % 2]
+            nc.vector.tensor_tensor(out=s1s[n][:, us, :], in0=pb[:, us, 0:512], in1=pb[:, us, 512:1024], op=ADD)
+            nc.vector.tensor_tensor(out=s2s[n][:, us, :], in0=s1s[n][:, us, 0:256], in1=s1s[n][:, us, 256:512], op=ADD)
+
+        def finish(n):
+            s2 = s2s[n]
+            t3 = small.tile([P, U, 128], F32, name="t3")
+            nc.vector.tensor_tensor(out=t3[:], in0=s2[:, :, 0:128], in1=s2[:, :, 128:256], op=ADD)
+            t4 = small.tile([P, U, 64], F32, name="t4")
+            nc.vector.tensor_tensor(out=t4[:], in0=t3[:, :, 0:64], in1=t3[:, :, 64:128], op=ADD)
+            t5 = small.tile([P, U, N], F32, name="t5")
+            nc.vector.tensor_tensor(out=t5[:], in0=t4[:, :, 0:N], in1=t4[:, :, N : 2 * N], op=ADD)
+            nc.vector.tensor_tensor(out=o_sb[:, n, :, :], in0=t5[:], in1=dgs[n][:], op=ADD)
+            nc.sync.dma_start(out=o_view[n], in_=o_sb[:, n, :, :].rearrange("p u c -> p (u c)"))
+
+        LAST = GROUPS - 1
+        transposes(0)
+        new_codes(0)
+        quantise_tile(0, 0)
+        quantise_tile(0, 1)
+        passes(0, 0)
+        passes(0, 1)
+        products(0, 0)
+        quantise_tile(0, 2)
+        quantise_tile(0, 3)
+        transposes(1)
+        products(0, 1)
+        pool_add1(0, 0)
+        passes(0, 2)
+        passes(0, 3)
+        products(0, 2)
+        products(0, 3)
+        pool_add1(0, 1)
+        diag_passes(0)
+        quantise(1)
+        load_group(3)
+        transposes(2)
+        diag_transposes(0)
+        diag_product(0)
+        pool_add2(0, slice(0, U))
+        for n in range(1, GROUPS):
+            if n + 3 < GROUPS:
+                load_group(n + 3)
+            diag_passes(n)
             for u in range(U):
-                h = ps_h.tile([P, 512], F32, name="h")
-                cols = slice(u * P, (u + 1) * P)
-                for i, (g, s) in enumerate(((0, 0), (0, 2), (1, 1), (1, 3))):
-                    nc.tensor.matmul_mx(
-                        out=h[:],
-                        lhsT=gcodes[:, g, cols].bitcast(E5X4),
-                        lhsT_scale=gscales[:, g, cols],
-                        rhs=mcodes[:, s, :].bitcast(E4X4),
-                        rhs_scale=mscales[:, s, :],
-                        start=(i == 0),
-                        stop=(i == 3),
-                    )
-                nc.vector.tensor_tensor(
-                    out=pb[:, u, 0:512].rearrange("p (d a) -> p d a", a=N),
-                    in0=h[:].rearrange("p (d a) -> p d a", a=N),
-                    in1=fper[:, u, 1 : 1 + 33 * 16].rearrange("p (d w) -> p d w", w=33)[:, :, 0:N],
-                    op=MULT,
-                )
-                nc.vector.tensor_tensor(
-                    out=pb[:, u, 513 : 513 + 33 * 15].rearrange("p (d w) -> p d w", w=33)[:, :, 0:N],
-                    in0=h[:, 0:480].rearrange("p (d a) -> p d a", a=N),
-                    in1=f_sb[:, grp, u, :].unsqueeze(1).to_broadcast([P, 15, N]),
-                    op=MULT,
-                )
-            nc.vector.tensor_reduce(
-                out=o_sb[:, grp, :, :],
-                in_=pb[:].rearrange("p u (r c) -> p u c r", c=N),
-                axis=AX,
-                op=ADD,
-            )
-            nc.sync.dma_start(out=o_view[grp], in_=o_sb[:, grp, :, :].rearrange("p u c -> p (u c)"))
+                passes(n, u)
+            diag_transposes(n)
+            if n + 2 < GROUPS:
+                transposes(n + 2)
+            products(n, 0)
+            products(n, 1)
+            pool_add1(n, 0)
+            if n + 1 < GROUPS:
+                quantise(n + 1)
+            products(n, 2)
+            products(n, 3)
+            diag_product(n)
+            finish(n - 1)
+            if n < LAST:
+                pool_add1(n, 1)
+                pool_add2(n, slice(0, U))
+            else:
+                pool_add2(n, slice(0, 2))
+                vector_adds(n, slice(2, U))
+        finish(LAST)

@@ -11,6 +11,7 @@ E4X4 = mybir.dt.float8_e4m3fn_x4
 E5X4 = mybir.dt.float8_e5m2_x4
 MULT = mybir.AluOpType.mult
 ADD = mybir.AluOpType.add
+AX = mybir.AxisListType.X
 
 P = 128
 Z, N, K = 4096, 32, 1024
@@ -53,7 +54,7 @@ def tile_tensorsquare_t_kernel(tc, features, mixing_matrix, grad_out, out):
         o_view = out.rearrange("(g p u) c -> g p (u c)", g=GROUPS, p=P, u=U)
         m_view = mixing_matrix.rearrange("(g w q e) c -> g w q e c", g=2, w=2, q=P, e=2)
 
-        graws, ggrs, gqs, fpers, dsbs, dtps, dgs, s1s, s2s, hs = {}, {}, {}, {}, {}, {}, {}, {}, {}, {}
+        graws, ggrs, gqs, fpers, dsbs, dtps, r1s, s1s, s2s, hs = {}, {}, {}, {}, {}, {}, {}, {}, {}, {}
 
         def load_group(n):
             graw = graw_pool.tile([P, U, K], BF16, name="graw")
@@ -171,10 +172,10 @@ def tile_tensorsquare_t_kernel(tc, features, mixing_matrix, grad_out, out):
                 nc.tensor.transpose(dtp[:, u, :], dsbs[n][:, u * P : (u + 1) * P], ident[:])
 
         def diag_product(n):
-            dg = small.tile([P, U, N], F32, name="dg")
-            dgs[n] = dg
+            r1 = small.tile([P, 3, U, N], F32, name="r1")
+            r1s[n] = r1
             nc.vector.scalar_tensor_tensor(
-                out=dg[:], in0=dtps[n][:, :, 0:N], scalar=2.0, in1=f_sb[:, n, :, :], op0=MULT, op1=MULT
+                out=r1[:, 2, :, :], in0=dtps[n][:, :, 0:N], scalar=2.0, in1=f_sb[:, n, :, :], op0=MULT, op1=MULT
             )
 
         def passes(n, u):
@@ -217,26 +218,34 @@ def tile_tensorsquare_t_kernel(tc, features, mixing_matrix, grad_out, out):
             pb = pbufs[n % 2]
             nc.gpsimd.tensor_tensor(out=s1s[n][:, us, :], in0=pb[:, us, 0:512], in1=pb[:, us, 512:1024], op=ADD)
 
-        def pool_add2(n, us):
+        def add2(eng, n, us):
             if n not in s2s:
-                s2 = small.tile([P, U, 256], F32, name="s2")
+                s2 = small.tile([P, 2, U, 128], F32, name="s2")
                 s2s[n] = s2
-            nc.gpsimd.tensor_tensor(out=s2s[n][:, us, :], in0=s1s[n][:, us, 0:256], in1=s1s[n][:, us, 256:512], op=ADD)
+            eng.tensor_tensor(
+                out=s2s[n][:, :, us, :].rearrange("p g u x -> p u g x"),
+                in0=s1s[n][:, us, 0:256].rearrange("p u (g x) -> p u g x", g=2),
+                in1=s1s[n][:, us, 256:512].rearrange("p u (g x) -> p u g x", g=2),
+                op=ADD,
+            )
+
+        def pool_add2(n, us):
+            add2(nc.gpsimd, n, us)
 
         def vector_adds(n, us):
             pb = pbufs[n % 2]
             nc.vector.tensor_tensor(out=s1s[n][:, us, :], in0=pb[:, us, 0:512], in1=pb[:, us, 512:1024], op=ADD)
-            nc.vector.tensor_tensor(out=s2s[n][:, us, :], in0=s1s[n][:, us, 0:256], in1=s1s[n][:, us, 256:512], op=ADD)
+            add2(nc.vector, n, us)
 
         def finish(n):
-            s2 = s2s[n]
-            t3 = small.tile([P, U, 128], F32, name="t3")
-            nc.vector.tensor_tensor(out=t3[:], in0=s2[:, :, 0:128], in1=s2[:, :, 128:256], op=ADD)
-            t4 = small.tile([P, U, 64], F32, name="t4")
-            nc.vector.tensor_tensor(out=t4[:], in0=t3[:, :, 0:64], in1=t3[:, :, 64:128], op=ADD)
-            t5 = small.tile([P, U, N], F32, name="t5")
-            nc.vector.tensor_tensor(out=t5[:], in0=t4[:, :, 0:N], in1=t4[:, :, N : 2 * N], op=ADD)
-            nc.vector.tensor_tensor(out=o_sb[:, n, :, :], in0=t5[:], in1=dgs[n][:], op=ADD)
+            r1 = r1s[n]
+            nc.vector.tensor_reduce(
+                out=r1[:, 0:2, :, :].rearrange("p g u c -> p (g u) c"),
+                in_=s2s[n][:].rearrange("p g u (r c) -> p (g u) c r", c=N),
+                axis=AX,
+                op=ADD,
+            )
+            nc.vector.tensor_reduce(out=o_sb[:, n, :, :], in_=r1[:].rearrange("p r u c -> p u c r"), axis=AX, op=ADD)
             nc.sync.dma_start(out=o_view[n], in_=o_sb[:, n, :, :].rearrange("p u c -> p (u c)"))
 
         LAST = GROUPS - 1
@@ -274,10 +283,10 @@ def tile_tensorsquare_t_kernel(tc, features, mixing_matrix, grad_out, out):
             if n + 2 < GROUPS:
                 transposes(n + 2)
             products(n, 0)
-            products(n, 1)
-            pool_add1(n, 0)
             if n + 1 < GROUPS:
                 quantise(n + 1)
+            products(n, 1)
+            pool_add1(n, 0)
             products(n, 2)
             products(n, 3)
             diag_product(n)

@@ -18,7 +18,7 @@ Z, N, K = 4096, 32, 1024
 GROUPS = 8
 U = 4
 FLOPS = 2 * Z * K * N * N + 4 * Z * N * N
-MANUAL = True
+V_SHARE = 5
 
 
 def tile_tensorsquare_t_kernel(tc, features, mixing_matrix, grad_out, out):
@@ -31,18 +31,14 @@ def tile_tensorsquare_t_kernel(tc, features, mixing_matrix, grad_out, out):
         gq_pool = ctx.enter_context(tc.tile_pool(name="gq", bufs=3))
         fper_pool = ctx.enter_context(tc.tile_pool(name="fperp", bufs=3))
         small = ctx.enter_context(tc.tile_pool(name="small", bufs=2))
-        ps_xt = ctx.enter_context(tc.psum_pool(name="psxt", bufs=3))
-        ps_h = ctx.enter_context(tc.psum_pool(name="psh", bufs=3))
+        ps_xt = ctx.enter_context(tc.psum_pool(name="psxt", bufs=2))
+        ps_h = ctx.enter_context(tc.psum_pool(name="psh", bufs=4))
         ps_d = ctx.enter_context(tc.psum_pool(name="psd", bufs=1))
         ps_dt = ctx.enter_context(tc.psum_pool(name="psdt", bufs=1))
-        if MANUAL:
-            ctx.enter_context(tc.manual_schedule())
+        ctx.enter_context(tc.manual_schedule())
 
         ident = keep.tile([P, P], F32, name="ident")
         make_identity(nc, ident[:])
-        pbufs = [keep.tile([P, U, 1024], F32, name="pbuf%d" % i) for i in range(2)]
-        for pb in pbufs:
-            nc.vector.memset(pb[:, :, 512:1024], 0.0)
         f_sb = keep.tile([P, GROUPS, U, N], BF16, name="f_sb")
         o_sb = keep.tile([P, GROUPS, U, N], F32, name="o_sb")
         mcodes = keep.tile([P, 4, 512], U32, name="mcodes", align_bytes=64)
@@ -54,24 +50,32 @@ def tile_tensorsquare_t_kernel(tc, features, mixing_matrix, grad_out, out):
         o_view = out.rearrange("(g p u) c -> g p (u c)", g=GROUPS, p=P, u=U)
         m_view = mixing_matrix.rearrange("(g w q e) c -> g w q e c", g=2, w=2, q=P, e=2)
 
-        graws, ggrs, gqs, fpers, dsbs, dtps, r1s, s1s, s2s, hs = {}, {}, {}, {}, {}, {}, {}, {}, {}, {}
+        graws, ggrs, gqs, fpers, dsbs, dtps, pbs, r1s, s1s, s2s, hs = {}, {}, {}, {}, {}, {}, {}, {}, {}, {}, {}
 
         def load_group(n):
             graw = graw_pool.tile([P, U, K], BF16, name="graw")
             nc.sync.dma_start(out=graw[:].rearrange("p u k -> p (u k)"), in_=g_view[n])
             graws[n] = graw
 
-        mraw = mprep.tile([P, 2, 4, 1536], BF16, name="mraw")
-        for g in range(2):
-            for w in range(2):
-                nc.sync.dma_start(out=mraw[:, g, 2 * w : 2 * w + 2, 0:1024], in_=m_view[g, w])
-        load_group(0)
+        def periodic_features(n):
+            fper = fper_pool.tile([P, U, 17 * N], BF16, name="fper")
+            fpers[n] = fper
+            nc.scalar.copy(
+                out=fper[:].rearrange("p u (r j) -> p u r j", j=N),
+                in_=f_sb[:, n, :, :].unsqueeze(2).to_broadcast([P, U, 17, N]),
+            )
+
         nc.sync.dma_start(
             out=f_sb[:].rearrange("p g u j -> p g (u j)"),
             in_=features.rearrange("(g p u) j -> p g (u j)", g=GROUPS, p=P, u=U),
         )
-        load_group(1)
-        load_group(2)
+        mraw = mprep.tile([P, 2, 4, 1536], BF16, name="mraw")
+        for g in range(2):
+            for w in range(2):
+                nc.sync.dma_start(out=mraw[:, g, 2 * w : 2 * w + 2, 0:1024], in_=m_view[g, w])
+        for n in range(3):
+            load_group(n)
+        periodic_features(0)
 
         msw = mprep.tile([P, 2, 4, 544], BF16, name="msw")
         mgr = mprep.tile([P, 4, 512 * 4], BF16, name="mgr", align_bytes=64)
@@ -81,10 +85,11 @@ def tile_tensorsquare_t_kernel(tc, features, mixing_matrix, grad_out, out):
             nc.vector.tensor_copy(out=mraw[:, g, :, 1024:1536], in_=mraw[:, g, :, 0:512])
             dst2 = mgr[:, 2 + g, :].rearrange("q (d a t) -> q d a t", a=N, t=4)
             for d in range(1, 17):
-                nc.scalar.copy(
-                    out=dst2[:, d - 1, :, :],
-                    in_=mraw[:, g, :, 32 * d : 32 * d + 33 * 31 + 1 : 33].rearrange("q t a -> q a t"),
-                )
+                src2 = mraw[:, g, :, 32 * d : 32 * d + 33 * 31 + 1 : 33].rearrange("q t a -> q a t")
+                if d <= V_SHARE:
+                    nc.vector.tensor_copy(out=dst2[:, d - 1, :, :], in_=src2)
+                else:
+                    nc.scalar.copy(out=dst2[:, d - 1, :, :], in_=src2)
             rows_hi = mraw[:, g, :, 512:1024].rearrange("q t (a h x) -> q t a h x", h=2, x=16)
             sw = msw[:, g, :, 0:512].rearrange("q t (a h x) -> q t a h x", h=2, x=16)
             nc.vector.tensor_copy(out=sw[:, :, :, 0, :], in_=rows_hi[:, :, :, 1, :])
@@ -117,12 +122,6 @@ def tile_tensorsquare_t_kernel(tc, features, mixing_matrix, grad_out, out):
                 for b in range(4):
                     nc.tensor.transpose(xt[:, b, :], words[:, b * P : (b + 1) * P], ident[:])
                 nc.scalar.copy(out=ggr_w[:, :, u, :, :], in_=xt[:].rearrange("q (g w) z -> q g z w", w=2))
-            fper = fper_pool.tile([P, U, 17 * N], BF16, name="fper")
-            fpers[n] = fper
-            nc.scalar.copy(
-                out=fper[:].rearrange("p u (r j) -> p u r j", j=N),
-                in_=f_sb[:, n, :, :].unsqueeze(2).to_broadcast([P, U, 17, N]),
-            )
 
         def new_codes(n):
             gcodes = gq_pool.tile([P, 2, 512], U32, name="gcodes", align_bytes=64)
@@ -141,12 +140,11 @@ def tile_tensorsquare_t_kernel(tc, features, mixing_matrix, grad_out, out):
         def quantise(n):
             new_codes(n)
             gcodes, gscales = gqs[n]
-            for g in range(2):
-                nc.vector.quantize_mx(
-                    out=gcodes[:, g, :].bitcast(E5X4),
-                    scales=gscales[:, g, :],
-                    in_=ggrs[n][:, g * 2048 : (g + 1) * 2048],
-                )
+            nc.vector.quantize_mx(
+                out=gcodes[:].rearrange("q g s -> q (g s)").bitcast(E5X4),
+                scales=gscales[:].rearrange("q g s -> q (g s)"),
+                in_=ggrs[n][:],
+            )
 
         def diag_passes(n):
             gcodes, gscales = gqs[n]
@@ -171,11 +169,14 @@ def tile_tensorsquare_t_kernel(tc, features, mixing_matrix, grad_out, out):
             for u in range(U):
                 nc.tensor.transpose(dtp[:, u, :], dsbs[n][:, u * P : (u + 1) * P], ident[:])
 
-        def diag_product(n):
-            r1 = small.tile([P, 3, U, N], F32, name="r1")
-            r1s[n] = r1
+        def diag_product(n, part):
+            pb = pbs[n]
+            if part == 0:
+                dst, cs = pb[:, :, 512 : 512 + 33 * 14 + 1 : 33], slice(0, 15)
+            else:
+                dst, cs = pb[:, :, 1007:1024], slice(15, N)
             nc.vector.scalar_tensor_tensor(
-                out=r1[:, 2, :, :], in0=dtps[n][:, :, 0:N], scalar=2.0, in1=f_sb[:, n, :, :], op0=MULT, op1=MULT
+                out=dst, in0=dtps[n][:, :, cs], scalar=2.0, in1=f_sb[:, n, :, cs], op0=MULT, op1=MULT
             )
 
         def passes(n, u):
@@ -195,7 +196,10 @@ def tile_tensorsquare_t_kernel(tc, features, mixing_matrix, grad_out, out):
                 )
 
         def products(n, u):
-            pb = pbufs[n % 2]
+            if n not in pbs:
+                pb_new = small.tile([P, U, 1024], F32, name="pb")
+                pbs[n] = pb_new
+            pb = pbs[n]
             h = hs[(n, u)]
             nc.vector.tensor_tensor(
                 out=pb[:, u, 0:512].rearrange("p (d a) -> p d a", a=N),
@@ -210,18 +214,14 @@ def tile_tensorsquare_t_kernel(tc, features, mixing_matrix, grad_out, out):
                 op=MULT,
             )
 
-        def pool_add1(n, half):
-            if half == 0:
+        def adds(eng, n, us):
+            if n not in s1s:
                 s1 = small.tile([P, U, 512], F32, name="s1")
                 s1s[n] = s1
-            us = slice(2 * half, 2 * half + 2)
-            pb = pbufs[n % 2]
-            nc.gpsimd.tensor_tensor(out=s1s[n][:, us, :], in0=pb[:, us, 0:512], in1=pb[:, us, 512:1024], op=ADD)
-
-        def add2(eng, n, us):
-            if n not in s2s:
                 s2 = small.tile([P, 2, U, 128], F32, name="s2")
                 s2s[n] = s2
+            pb = pbs[n]
+            eng.tensor_tensor(out=s1s[n][:, us, :], in0=pb[:, us, 0:512], in1=pb[:, us, 512:1024], op=ADD)
             eng.tensor_tensor(
                 out=s2s[n][:, :, us, :].rearrange("p g u x -> p u g x"),
                 in0=s1s[n][:, us, 0:256].rearrange("p u (g x) -> p u g x", g=2),
@@ -229,18 +229,10 @@ def tile_tensorsquare_t_kernel(tc, features, mixing_matrix, grad_out, out):
                 op=ADD,
             )
 
-        def pool_add2(n, us):
-            add2(nc.gpsimd, n, us)
-
-        def vector_adds(n, us):
-            pb = pbufs[n % 2]
-            nc.vector.tensor_tensor(out=s1s[n][:, us, :], in0=pb[:, us, 0:512], in1=pb[:, us, 512:1024], op=ADD)
-            add2(nc.vector, n, us)
-
         def finish(n):
-            r1 = r1s[n]
+            r1 = small.tile([P, 2, U, N], F32, name="r1")
             nc.vector.tensor_reduce(
-                out=r1[:, 0:2, :, :].rearrange("p g u c -> p (g u) c"),
+                out=r1[:].rearrange("p g u c -> p (g u) c"),
                 in_=s2s[n][:].rearrange("p g u (r c) -> p (g u) c r", c=N),
                 axis=AX,
                 op=ADD,
@@ -249,6 +241,7 @@ def tile_tensorsquare_t_kernel(tc, features, mixing_matrix, grad_out, out):
             nc.sync.dma_start(out=o_view[n], in_=o_sb[:, n, :, :].rearrange("p u c -> p (u c)"))
 
         LAST = GROUPS - 1
+        ALL = slice(0, U)
         transposes(0)
         new_codes(0)
         quantise_tile(0, 0)
@@ -259,21 +252,23 @@ def tile_tensorsquare_t_kernel(tc, features, mixing_matrix, grad_out, out):
         quantise_tile(0, 2)
         quantise_tile(0, 3)
         transposes(1)
-        products(0, 1)
-        pool_add1(0, 0)
+        periodic_features(1)
+        diag_passes(0)
         passes(0, 2)
         passes(0, 3)
-        products(0, 2)
-        products(0, 3)
-        pool_add1(0, 1)
-        diag_passes(0)
-        quantise(1)
+        diag_transposes(0)
         load_group(3)
         transposes(2)
-        diag_transposes(0)
-        diag_product(0)
-        pool_add2(0, slice(0, U))
-        for n in range(1, GROUPS):
+        periodic_features(2)
+        products(0, 1)
+        quantise(1)
+        products(0, 2)
+        products(0, 3)
+        diag_product(0, 0)
+        quantise(2)
+        diag_product(0, 1)
+        adds(nc.gpsimd, 0, ALL)
+        for n in range(1, LAST):
             if n + 3 < GROUPS:
                 load_group(n + 3)
             diag_passes(n)
@@ -282,19 +277,26 @@ def tile_tensorsquare_t_kernel(tc, features, mixing_matrix, grad_out, out):
             diag_transposes(n)
             if n + 2 < GROUPS:
                 transposes(n + 2)
-            products(n, 0)
-            if n + 1 < GROUPS:
-                quantise(n + 1)
-            products(n, 1)
-            pool_add1(n, 0)
-            products(n, 2)
-            products(n, 3)
-            diag_product(n)
+                periodic_features(n + 2)
+            for u in range(U):
+                products(n, u)
+            diag_product(n, 0)
+            if n + 2 < GROUPS:
+                quantise(n + 2)
+            diag_product(n, 1)
+            adds(nc.gpsimd, n, ALL)
             finish(n - 1)
-            if n < LAST:
-                pool_add1(n, 1)
-                pool_add2(n, slice(0, U))
-            else:
-                pool_add2(n, slice(0, 2))
-                vector_adds(n, slice(2, U))
+        diag_passes(LAST)
+        for u in range(U):
+            passes(LAST, u)
+        diag_transposes(LAST)
+        products(LAST, 0)
+        diag_product(LAST, 0)
+        diag_product(LAST, 1)
+        products(LAST, 1)
+        adds(nc.gpsimd, LAST, slice(0, 2))
+        products(LAST, 2)
+        products(LAST, 3)
+        finish(LAST - 1)
+        adds(nc.vector, LAST, slice(2, U))
         finish(LAST)

@@ -18,7 +18,7 @@ Z, N, K = 4096, 32, 1024
 GROUPS = 8
 U = 4
 FLOPS = 2 * Z * K * N * N + 4 * Z * N * N
-V_SHARE = 5
+V_SHARE = 4
 
 
 def tile_tensorsquare_t_kernel(tc, features, mixing_matrix, grad_out, out):
@@ -57,13 +57,15 @@ def tile_tensorsquare_t_kernel(tc, features, mixing_matrix, grad_out, out):
             nc.sync.dma_start(out=graw[:].rearrange("p u k -> p (u k)"), in_=g_view[n])
             graws[n] = graw
 
-        def periodic_features(n):
+        def periodic_features(n, on_vector=False):
             fper = fper_pool.tile([P, U, 17 * N], BF16, name="fper")
             fpers[n] = fper
-            nc.scalar.copy(
-                out=fper[:].rearrange("p u (r j) -> p u r j", j=N),
-                in_=f_sb[:, n, :, :].unsqueeze(2).to_broadcast([P, U, 17, N]),
-            )
+            dst = fper[:].rearrange("p u (r j) -> p u r j", j=N)
+            src = f_sb[:, n, :, :].unsqueeze(2).to_broadcast([P, U, 17, N])
+            if on_vector:
+                nc.vector.tensor_copy(out=dst, in_=src)
+            else:
+                nc.scalar.copy(out=dst, in_=src)
 
         nc.sync.dma_start(
             out=f_sb[:].rearrange("p g u j -> p g (u j)"),
@@ -238,29 +240,30 @@ def tile_tensorsquare_t_kernel(tc, features, mixing_matrix, grad_out, out):
                 op=ADD,
             )
             nc.vector.tensor_reduce(out=o_sb[:, n, :, :], in_=r1[:].rearrange("p r u c -> p u c r"), axis=AX, op=ADD)
-            nc.sync.dma_start(out=o_view[n], in_=o_sb[:, n, :, :].rearrange("p u c -> p (u c)"))
+            first_store = GROUPS - 4
+            if n >= first_store:
+                for m in range(0 if n == first_store else n, n + 1):
+                    nc.sync.dma_start(out=o_view[m], in_=o_sb[:, m, :, :].rearrange("p u c -> p (u c)"))
 
         LAST = GROUPS - 1
         ALL = slice(0, U)
         transposes(0)
         new_codes(0)
-        quantise_tile(0, 0)
-        quantise_tile(0, 1)
+        for u in range(U):
+            quantise_tile(0, u)
+        periodic_features(1, on_vector=True)
         passes(0, 0)
         passes(0, 1)
-        products(0, 0)
-        quantise_tile(0, 2)
-        quantise_tile(0, 3)
         transposes(1)
-        periodic_features(1)
-        diag_passes(0)
         passes(0, 2)
         passes(0, 3)
-        diag_transposes(0)
+        diag_passes(0)
         load_group(3)
         transposes(2)
-        periodic_features(2)
+        diag_transposes(0)
+        products(0, 0)
         products(0, 1)
+        periodic_features(2, on_vector=True)
         quantise(1)
         products(0, 2)
         products(0, 3)
@@ -293,10 +296,9 @@ def tile_tensorsquare_t_kernel(tc, features, mixing_matrix, grad_out, out):
         products(LAST, 0)
         diag_product(LAST, 0)
         diag_product(LAST, 1)
-        products(LAST, 1)
-        adds(nc.gpsimd, LAST, slice(0, 2))
-        products(LAST, 2)
-        products(LAST, 3)
+        for u in range(1, U):
+            products(LAST, u)
+        adds(nc.gpsimd, LAST, slice(0, 1))
         finish(LAST - 1)
-        adds(nc.vector, LAST, slice(2, U))
+        adds(nc.vector, LAST, slice(1, U))
         finish(LAST)

@@ -114,11 +114,12 @@ def tile_tensorsquare_t_kernel(tc, features, mixing_matrix, grad_out, out):
         )
         nc.vector.quantize_mx(out=mcodes[:, 3, :].bitcast(E4X4), scales=mscales[:, 3, :], in_=mgr[:, 3, :])
 
-        def transposes(n):
-            ggr = ggr_pool.tile([P, 2 * U * P * 4], BF16, name="ggr", align_bytes=64)
-            ggrs[n] = ggr
-            ggr_w = ggr[:].bitcast(F32).rearrange("q (g u z w) -> q g u z w", g=2, u=U, z=P, w=2)
-            for u in range(U):
+        def transposes(n, us):
+            if n not in ggrs:
+                ggr_new = ggr_pool.tile([P, 2 * U * P * 4], BF16, name="ggr", align_bytes=64)
+                ggrs[n] = ggr_new
+            ggr_w = ggrs[n][:].bitcast(F32).rearrange("q (g u z w) -> q g u z w", g=2, u=U, z=P, w=2)
+            for u in us:
                 xt = ps_xt.tile([P, 4, P], F32, name="xt")
                 words = graws[n][:, u, :].bitcast(F32)
                 for b in range(4):
@@ -247,20 +248,22 @@ def tile_tensorsquare_t_kernel(tc, features, mixing_matrix, grad_out, out):
 
         LAST = GROUPS - 1
         ALL = slice(0, U)
-        transposes(0)
+        transposes(0, (0, 1, 2, 3))
         new_codes(0)
         for u in range(U):
             quantise_tile(0, u)
         periodic_features(1, on_vector=True)
         passes(0, 0)
+        transposes(1, (0, 1))
         passes(0, 1)
-        transposes(1)
-        passes(0, 2)
-        passes(0, 3)
         diag_passes(0)
+        transposes(1, (2, 3))
+        passes(0, 2)
         load_group(3)
-        transposes(2)
         diag_transposes(0)
+        transposes(2, (0, 1))
+        passes(0, 3)
+        transposes(2, (2, 3))
         products(0, 0)
         products(0, 1)
         periodic_features(2, on_vector=True)
@@ -272,19 +275,24 @@ def tile_tensorsquare_t_kernel(tc, features, mixing_matrix, grad_out, out):
         diag_product(0, 1)
         adds(nc.gpsimd, 0, ALL)
         for n in range(1, LAST):
+            more = n + 2 < GROUPS
             if n + 3 < GROUPS:
                 load_group(n + 3)
             diag_passes(n)
-            for u in range(U):
-                passes(n, u)
+            passes(n, 0)
+            passes(n, 1)
+            if more:
+                transposes(n + 2, (0, 1))
+            passes(n, 2)
+            passes(n, 3)
             diag_transposes(n)
-            if n + 2 < GROUPS:
-                transposes(n + 2)
+            if more:
+                transposes(n + 2, (2, 3))
                 periodic_features(n + 2)
             for u in range(U):
                 products(n, u)
             diag_product(n, 0)
-            if n + 2 < GROUPS:
+            if more:
                 quantise(n + 2)
             diag_product(n, 1)
             adds(nc.gpsimd, n, ALL)

@@ -67,7 +67,7 @@ def tile_tensorsquare_t_kernel(tc, features, mixing_matrix, grad_out, out):
             else:
                 nc.scalar.copy(out=dst, in_=src)
 
-        nc.sync.dma_start(
+        nc.scalar.dma_start(
             out=f_sb[:].rearrange("p g u j -> p g (u j)"),
             in_=features.rearrange("(g p u) j -> p g (u j)", g=GROUPS, p=P, u=U),
         )
@@ -101,18 +101,21 @@ def tile_tensorsquare_t_kernel(tc, features, mixing_matrix, grad_out, out):
             nc.vector.tensor_copy(out=dst[:, :, 0:16, :], in_=src_lo[:, 0:16, :, :])
             src_hi = msw[:, g, :, 1 : 1 + 33 * 16].rearrange("q t (a w) -> q w a t", w=33)
             nc.vector.tensor_copy(out=dst[:, :, 16:32, :], in_=src_hi[:, 0:16, :, :])
-            nc.vector.tensor_copy(
-                out=mgd[:, g, 0 : N * 4].rearrange("q (a t) -> q a t", t=4),
-                in_=mraw[:, g, :, 0 : 33 * 31 + 1 : 33].rearrange("q t a -> q a t"),
-            )
             nc.vector.quantize_mx(out=mcodes[:, g, :].bitcast(E4X4), scales=mscales[:, g, :], in_=mgr[:, g, :])
         nc.vector.quantize_mx(out=mcodes[:, 2, :].bitcast(E4X4), scales=mscales[:, 2, :], in_=mgr[:, 2, :])
-        nc.vector.quantize_mx(
-            out=dcodes[:].rearrange("q g s -> q (g s)").bitcast(E4X4),
-            scales=dscales[:].rearrange("q g s -> q (g s)"),
-            in_=mgd[:].rearrange("q g s -> q (g s)"),
-        )
         nc.vector.quantize_mx(out=mcodes[:, 3, :].bitcast(E4X4), scales=mscales[:, 3, :], in_=mgr[:, 3, :])
+
+        def prepare_diagonal():
+            for g in range(2):
+                nc.vector.tensor_copy(
+                    out=mgd[:, g, 0 : N * 4].rearrange("q (a t) -> q a t", t=4),
+                    in_=mraw[:, g, :, 0 : 33 * 31 + 1 : 33].rearrange("q t a -> q a t"),
+                )
+            nc.vector.quantize_mx(
+                out=dcodes[:].rearrange("q g s -> q (g s)").bitcast(E4X4),
+                scales=dscales[:].rearrange("q g s -> q (g s)"),
+                in_=mgd[:].rearrange("q g s -> q (g s)"),
+            )
 
         def transposes(n, us):
             if n not in ggrs:
@@ -172,14 +175,14 @@ def tile_tensorsquare_t_kernel(tc, features, mixing_matrix, grad_out, out):
             for u in range(U):
                 nc.tensor.transpose(dtp[:, u, :], dsbs[n][:, u * P : (u + 1) * P], ident[:])
 
-        def diag_product(n, part):
+        def diag_product(n, part, us=slice(0, U)):
             pb = pbs[n]
             if part == 0:
-                dst, cs = pb[:, :, 512 : 512 + 33 * 14 + 1 : 33], slice(0, 15)
+                dst, cs = pb[:, us, 512 : 512 + 33 * 14 + 1 : 33], slice(0, 15)
             else:
-                dst, cs = pb[:, :, 1007:1024], slice(15, N)
+                dst, cs = pb[:, us, 1007:1024], slice(15, N)
             nc.vector.scalar_tensor_tensor(
-                out=dst, in0=dtps[n][:, :, cs], scalar=2.0, in1=f_sb[:, n, :, cs], op0=MULT, op1=MULT
+                out=dst, in0=dtps[n][:, us, cs], scalar=2.0, in1=f_sb[:, n, us, cs], op0=MULT, op1=MULT
             )
 
         def passes(n, u):
@@ -253,6 +256,7 @@ def tile_tensorsquare_t_kernel(tc, features, mixing_matrix, grad_out, out):
         for u in range(U):
             quantise_tile(0, u)
         periodic_features(1, on_vector=True)
+        prepare_diagonal()
         passes(0, 0)
         transposes(1, (0, 1))
         passes(0, 1)
@@ -271,9 +275,11 @@ def tile_tensorsquare_t_kernel(tc, features, mixing_matrix, grad_out, out):
         products(0, 2)
         products(0, 3)
         diag_product(0, 0)
+        diag_product(0, 1, slice(0, 1))
+        adds(nc.vector, 0, slice(0, 1))
         quantise(2)
-        diag_product(0, 1)
-        adds(nc.gpsimd, 0, ALL)
+        diag_product(0, 1, slice(1, U))
+        adds(nc.gpsimd, 0, slice(1, U))
         for n in range(1, LAST):
             more = n + 2 < GROUPS
             if n + 3 < GROUPS:

@@ -45,6 +45,7 @@ def tile_tensorsquare_t_kernel(tc, features, mixing_matrix, grad_out, out):
         mscales = keep.tile([P, 4, 512], U8, name="mscales", align_bytes=64)
         dcodes = keep.tile([P, 2, P], U32, name="dcodes", align_bytes=64)
         dscales = keep.tile([P, 2, P], U8, name="dscales", align_bytes=64)
+        m2 = keep.tile([P, GROUPS, U, 512], BF16, name="m2")
 
         g_view = grad_out.rearrange("(g p u) k -> g p (u k)", g=GROUPS, p=P, u=U)
         o_view = out.rearrange("(g p u) c -> g p (u c)", g=GROUPS, p=P, u=U)
@@ -57,15 +58,19 @@ def tile_tensorsquare_t_kernel(tc, features, mixing_matrix, grad_out, out):
             nc.sync.dma_start(out=graw[:].rearrange("p u k -> p (u k)"), in_=g_view[n])
             graws[n] = graw
 
-        def periodic_features(n, on_vector=False):
-            fper = fper_pool.tile([P, U, 17 * N], BF16, name="fper")
+        def periodic_features(n, copy):
+            fper = fper_pool.tile([P, U, 16 * N], BF16, name="fper")
             fpers[n] = fper
-            dst = fper[:].rearrange("p u (r j) -> p u r j", j=N)
-            src = f_sb[:, n, :, :].unsqueeze(2).to_broadcast([P, U, 17, N])
-            if on_vector:
-                nc.vector.tensor_copy(out=dst, in_=src)
-            else:
-                nc.scalar.copy(out=dst, in_=src)
+            copy(
+                out=fper[:].bitcast(F32).rearrange("p u (r j) -> p u r j", j=N // 2),
+                in_=f_sb[:, n, :, :].bitcast(F32).unsqueeze(2).to_broadcast([P, U, 16, N // 2]),
+            )
+
+        def plain_features(n, copy):
+            copy(
+                out=m2[:, n, :, 0:495].rearrange("p u (s w) -> p u s w", w=33)[:, :, :, 1:33],
+                in_=f_sb[:, n, :, :].unsqueeze(2).to_broadcast([P, U, 15, N]),
+            )
 
         nc.scalar.dma_start(
             out=f_sb[:].rearrange("p g u j -> p g (u j)"),
@@ -77,7 +82,13 @@ def tile_tensorsquare_t_kernel(tc, features, mixing_matrix, grad_out, out):
                 nc.sync.dma_start(out=mraw[:, g, 2 * w : 2 * w + 2, 0:1024], in_=m_view[g, w])
         for n in range(3):
             load_group(n)
-        periodic_features(0)
+        periodic_features(0, nc.vector.tensor_copy)
+        periodic_features(1, nc.vector.tensor_copy)
+        m2_gu = m2[:].rearrange("p g u x -> p (g u) x")
+        f_gu = f_sb[:].rearrange("p g u j -> p (g u) j")
+        nc.scalar.copy(out=m2_gu[:, :, 0:496:33], in_=f_gu[:, :, 16:32])
+        nc.scalar.copy(out=m2_gu[:, :, 496:512], in_=f_gu[:, :, 0:16])
+        plain_features(0, nc.scalar.copy)
 
         msw = mprep.tile([P, 2, 4, 544], BF16, name="msw")
         mgr = mprep.tile([P, 4, 512 * 4], BF16, name="mgr", align_bytes=64)
@@ -85,22 +96,30 @@ def tile_tensorsquare_t_kernel(tc, features, mixing_matrix, grad_out, out):
         nc.gpsimd.memset(mgd[:], 0.0)
         for g in range(2):
             nc.vector.tensor_copy(out=mraw[:, g, :, 1024:1536], in_=mraw[:, g, :, 0:512])
-            dst2 = mgr[:, 2 + g, :].rearrange("q (d a t) -> q d a t", a=N, t=4)
-            for d in range(1, 17):
+            run_lo = mraw[:, g, :, 16 : 16 + 33 * 15 + 1 : 33].rearrange("q t a -> q a t")
+            run_hi = mraw[:, g, :, 512 : 512 + 33 * 15 + 1 : 33].rearrange("q t a -> q a t")
+            cols1 = mgr[:, g, :].rearrange("q (x t) -> q x t", t=4)
+            cols2 = mgr[:, 2 + g, :].rearrange("q (x t) -> q x t", t=4)
+            nc.scalar.copy(out=cols1[:, 0:496:33, :], in_=run_lo)
+            nc.scalar.copy(out=cols1[:, 496:512, :], in_=run_hi)
+            dst2 = mgr[:, 2 + g, 4:1984].rearrange("q (s w t) -> q s w t", w=33, t=4)
+            for d in range(1, 16):
                 src2 = mraw[:, g, :, 32 * d : 32 * d + 33 * 31 + 1 : 33].rearrange("q t a -> q a t")
                 if d <= V_SHARE:
-                    nc.vector.tensor_copy(out=dst2[:, d - 1, :, :], in_=src2)
+                    nc.vector.tensor_copy(out=dst2[:, d - 1, 0:N, :], in_=src2)
                 else:
-                    nc.scalar.copy(out=dst2[:, d - 1, :, :], in_=src2)
+                    nc.scalar.copy(out=dst2[:, d - 1, 0:N, :], in_=src2)
+            nc.scalar.copy(out=cols2[:, 0:496:33, :], in_=run_hi)
+            nc.scalar.copy(out=cols2[:, 496:512, :], in_=run_lo)
             rows_hi = mraw[:, g, :, 512:1024].rearrange("q t (a h x) -> q t a h x", h=2, x=16)
             sw = msw[:, g, :, 0:512].rearrange("q t (a h x) -> q t a h x", h=2, x=16)
             nc.vector.tensor_copy(out=sw[:, :, :, 0, :], in_=rows_hi[:, :, :, 1, :])
             nc.vector.tensor_copy(out=sw[:, :, :, 1, :], in_=rows_hi[:, :, :, 0, :])
-            dst = mgr[:, g, :].rearrange("q (d a t) -> q d a t", a=N, t=4)
+            dst = mgr[:, g, 4:1984].rearrange("q (s w t) -> q s w t", w=33, t=4)
             src_lo = mraw[:, g, :, 1 : 1 + 33 * 16].rearrange("q t (a w) -> q w a t", w=33)
-            nc.vector.tensor_copy(out=dst[:, :, 0:16, :], in_=src_lo[:, 0:16, :, :])
+            nc.vector.tensor_copy(out=dst[:, :, 0:16, :], in_=src_lo[:, 0:15, :, :])
             src_hi = msw[:, g, :, 1 : 1 + 33 * 16].rearrange("q t (a w) -> q w a t", w=33)
-            nc.vector.tensor_copy(out=dst[:, :, 16:32, :], in_=src_hi[:, 0:16, :, :])
+            nc.vector.tensor_copy(out=dst[:, :, 16:32, :], in_=src_hi[:, 0:15, :, :])
             nc.vector.quantize_mx(out=mcodes[:, g, :].bitcast(E4X4), scales=mscales[:, g, :], in_=mgr[:, g, :])
         nc.vector.quantize_mx(out=mcodes[:, 2, :].bitcast(E4X4), scales=mscales[:, 2, :], in_=mgr[:, 2, :])
         nc.vector.quantize_mx(out=mcodes[:, 3, :].bitcast(E4X4), scales=mscales[:, 3, :], in_=mgr[:, 3, :])
@@ -175,14 +194,9 @@ def tile_tensorsquare_t_kernel(tc, features, mixing_matrix, grad_out, out):
             for u in range(U):
                 nc.tensor.transpose(dtp[:, u, :], dsbs[n][:, u * P : (u + 1) * P], ident[:])
 
-        def diag_product(n, part, us=slice(0, U)):
-            pb = pbs[n]
-            if part == 0:
-                dst, cs = pb[:, us, 512 : 512 + 33 * 14 + 1 : 33], slice(0, 15)
-            else:
-                dst, cs = pb[:, us, 1007:1024], slice(15, N)
+        def diag_product(n, us=slice(0, U)):
             nc.vector.scalar_tensor_tensor(
-                out=dst, in0=dtps[n][:, us, cs], scalar=2.0, in1=f_sb[:, n, us, cs], op0=MULT, op1=MULT
+                out=pbs[n][:, us, 480:512], in0=dtps[n][:, us, 0:N], scalar=2.0, in1=f_sb[:, n, us, :], op0=MULT, op1=MULT
             )
 
         def passes(n, u):
@@ -208,17 +222,12 @@ def tile_tensorsquare_t_kernel(tc, features, mixing_matrix, grad_out, out):
             pb = pbs[n]
             h = hs[(n, u)]
             nc.vector.tensor_tensor(
-                out=pb[:, u, 0:512].rearrange("p (d a) -> p d a", a=N),
-                in0=h[:].rearrange("p (d a) -> p d a", a=N),
-                in1=fpers[n][:, u, 1 : 1 + 33 * 16].rearrange("p (d w) -> p d w", w=33)[:, :, 0:N],
+                out=pb[:, u, 0:480].rearrange("p (s a) -> p s a", a=N),
+                in0=h[:, 1:496].rearrange("p (s w) -> p s w", w=33)[:, :, 0:N],
+                in1=fpers[n][:, u, 1:496].rearrange("p (s w) -> p s w", w=33)[:, :, 0:N],
                 op=MULT,
             )
-            nc.vector.tensor_tensor(
-                out=pb[:, u, 513 : 513 + 33 * 15].rearrange("p (d w) -> p d w", w=33)[:, :, 0:N],
-                in0=h[:, 0:480].rearrange("p (d a) -> p d a", a=N),
-                in1=f_sb[:, n, u, :].unsqueeze(1).to_broadcast([P, 15, N]),
-                op=MULT,
-            )
+            nc.vector.tensor_tensor(out=pb[:, u, 512:1024], in0=h[:], in1=m2[:, n, u, :], op=MULT)
 
         def adds(eng, n, us):
             if n not in s1s:
@@ -255,7 +264,6 @@ def tile_tensorsquare_t_kernel(tc, features, mixing_matrix, grad_out, out):
         new_codes(0)
         for u in range(U):
             quantise_tile(0, u)
-        periodic_features(1, on_vector=True)
         prepare_diagonal()
         passes(0, 0)
         transposes(1, (0, 1))
@@ -268,17 +276,18 @@ def tile_tensorsquare_t_kernel(tc, features, mixing_matrix, grad_out, out):
         transposes(2, (0, 1))
         passes(0, 3)
         transposes(2, (2, 3))
+        plain_features(1, nc.scalar.copy)
+        periodic_features(2, nc.scalar.copy)
+        plain_features(2, nc.scalar.copy)
         products(0, 0)
         products(0, 1)
-        periodic_features(2, on_vector=True)
         quantise(1)
         products(0, 2)
         products(0, 3)
-        diag_product(0, 0)
-        diag_product(0, 1, slice(0, 1))
+        diag_product(0, slice(0, 1))
         adds(nc.vector, 0, slice(0, 1))
         quantise(2)
-        diag_product(0, 1, slice(1, U))
+        diag_product(0, slice(1, U))
         adds(nc.gpsimd, 0, slice(1, U))
         for n in range(1, LAST):
             more = n + 2 < GROUPS
@@ -294,13 +303,13 @@ def tile_tensorsquare_t_kernel(tc, features, mixing_matrix, grad_out, out):
             diag_transposes(n)
             if more:
                 transposes(n + 2, (2, 3))
-                periodic_features(n + 2)
+                periodic_features(n + 2, nc.scalar.copy)
+                plain_features(n + 2, nc.scalar.copy)
             for u in range(U):
                 products(n, u)
-            diag_product(n, 0)
             if more:
                 quantise(n + 2)
-            diag_product(n, 1)
+            diag_product(n)
             adds(nc.gpsimd, n, ALL)
             finish(n - 1)
         diag_passes(LAST)
@@ -308,8 +317,7 @@ def tile_tensorsquare_t_kernel(tc, features, mixing_matrix, grad_out, out):
             passes(LAST, u)
         diag_transposes(LAST)
         products(LAST, 0)
-        diag_product(LAST, 0)
-        diag_product(LAST, 1)
+        diag_product(LAST)
         for u in range(1, U):
             products(LAST, u)
         adds(nc.gpsimd, LAST, slice(0, 1))

@@ -18,7 +18,6 @@ Z, N, K = 4096, 32, 1024
 GROUPS = 8
 U = 4
 FLOPS = 2 * Z * K * N * N + 4 * Z * N * N
-V_SHARE = 4
 
 
 def tile_tensorsquare_t_kernel(tc, features, mixing_matrix, grad_out, out):
@@ -39,6 +38,8 @@ def tile_tensorsquare_t_kernel(tc, features, mixing_matrix, grad_out, out):
 
         ident = keep.tile([P, P], F32, name="ident")
         make_identity(nc, ident[:])
+        identb = keep.tile([P, P], BF16, name="identb")
+        make_identity(nc, identb[:])
         f_sb = keep.tile([P, GROUPS, U, N], BF16, name="f_sb")
         o_sb = keep.tile([P, GROUPS, U, N], F32, name="o_sb")
         mcodes = keep.tile([P, 4, 512], U32, name="mcodes", align_bytes=64)
@@ -83,7 +84,6 @@ def tile_tensorsquare_t_kernel(tc, features, mixing_matrix, grad_out, out):
         for n in range(3):
             load_group(n)
         periodic_features(0, nc.vector.tensor_copy)
-        periodic_features(1, nc.vector.tensor_copy)
         m2_gu = m2[:].rearrange("p g u x -> p (g u) x")
         f_gu = f_sb[:].rearrange("p g u j -> p (g u) j")
         nc.scalar.copy(out=m2_gu[:, :, 0:496:33], in_=f_gu[:, :, 16:32])
@@ -94,35 +94,58 @@ def tile_tensorsquare_t_kernel(tc, features, mixing_matrix, grad_out, out):
         mgr = mprep.tile([P, 4, 512 * 4], BF16, name="mgr", align_bytes=64)
         mgd = mprep.tile([P, 2, P * 4], BF16, name="mgd", align_bytes=64)
         nc.gpsimd.memset(mgd[:], 0.0)
+
+        def permute(dst, src):
+            nc.tensor.matmul(out=dst, lhsT=identb[:], rhs=src, start=True, stop=True)
+
+        def by_column(ap):
+            return ap.rearrange("q (a t) -> q a t", t=4)
+
         for g in range(2):
             nc.vector.tensor_copy(out=mraw[:, g, :, 1024:1536], in_=mraw[:, g, :, 0:512])
-            run_lo = mraw[:, g, :, 16 : 16 + 33 * 15 + 1 : 33].rearrange("q t a -> q a t")
-            run_hi = mraw[:, g, :, 512 : 512 + 33 * 15 + 1 : 33].rearrange("q t a -> q a t")
-            cols1 = mgr[:, g, :].rearrange("q (x t) -> q x t", t=4)
-            cols2 = mgr[:, 2 + g, :].rearrange("q (x t) -> q x t", t=4)
-            nc.scalar.copy(out=cols1[:, 0:496:33, :], in_=run_lo)
-            nc.scalar.copy(out=cols1[:, 496:512, :], in_=run_hi)
-            dst2 = mgr[:, 2 + g, 4:1984].rearrange("q (s w t) -> q s w t", w=33, t=4)
-            for d in range(1, 16):
-                src2 = mraw[:, g, :, 32 * d : 32 * d + 33 * 31 + 1 : 33].rearrange("q t a -> q a t")
-                if d <= V_SHARE:
-                    nc.vector.tensor_copy(out=dst2[:, d - 1, 0:N, :], in_=src2)
-                else:
-                    nc.scalar.copy(out=dst2[:, d - 1, 0:N, :], in_=src2)
-            nc.scalar.copy(out=cols2[:, 0:496:33, :], in_=run_hi)
-            nc.scalar.copy(out=cols2[:, 496:512, :], in_=run_lo)
             rows_hi = mraw[:, g, :, 512:1024].rearrange("q t (a h x) -> q t a h x", h=2, x=16)
             sw = msw[:, g, :, 0:512].rearrange("q t (a h x) -> q t a h x", h=2, x=16)
             nc.vector.tensor_copy(out=sw[:, :, :, 0, :], in_=rows_hi[:, :, :, 1, :])
             nc.vector.tensor_copy(out=sw[:, :, :, 1, :], in_=rows_hi[:, :, :, 0, :])
-            dst = mgr[:, g, 4:1984].rearrange("q (s w t) -> q s w t", w=33, t=4)
+        for g in range(2):
+            run_lo = mraw[:, g, :, 16 : 16 + 33 * 15 + 1 : 33].rearrange("q t a -> q a t")
+            run_hi = mraw[:, g, :, 512 : 512 + 33 * 15 + 1 : 33].rearrange("q t a -> q a t")
             src_lo = mraw[:, g, :, 1 : 1 + 33 * 16].rearrange("q t (a w) -> q w a t", w=33)
-            nc.vector.tensor_copy(out=dst[:, :, 0:16, :], in_=src_lo[:, 0:15, :, :])
             src_hi = msw[:, g, :, 1 : 1 + 33 * 16].rearrange("q t (a w) -> q w a t", w=33)
-            nc.vector.tensor_copy(out=dst[:, :, 16:32, :], in_=src_hi[:, 0:15, :, :])
-            nc.vector.quantize_mx(out=mcodes[:, g, :].bitcast(E4X4), scales=mscales[:, g, :], in_=mgr[:, g, :])
-        nc.vector.quantize_mx(out=mcodes[:, 2, :].bitcast(E4X4), scales=mscales[:, 2, :], in_=mgr[:, 2, :])
-        nc.vector.quantize_mx(out=mcodes[:, 3, :].bitcast(E4X4), scales=mscales[:, 3, :], in_=mgr[:, 3, :])
+            for source in range(2):
+                b0 = ps_h.tile([P, 1024], BF16, name="h")
+                b1 = ps_h.tile([P, 1024], BF16, name="h")
+                r0 = b0[:, 4:928].rearrange("q (s w t) -> q s w t", w=33, t=4)
+                r1 = b1[:, 36:960].rearrange("q (s w t) -> q s w t", w=33, t=4)
+                first, second = (run_lo, run_hi) if source == 0 else (run_hi, run_lo)
+                permute(by_column(b0[:])[:, 0:232:33, :], first[:, 0:8, :])
+                permute(by_column(b1[:])[:, 8:240:33, :], first[:, 8:16, :])
+                permute(by_column(b1[:, 960:1024]), second)
+                if source == 0:
+                    permute(r0[:, :, 0:16, :], src_lo[:, 0:7, :, :])
+                    permute(by_column(b0[:, 928:992]), src_lo[:, 7, :, :])
+                    permute(r1[:, :, 0:16, :], src_lo[:, 8:15, :, :])
+                    permute(r0[:, :, 16:32, :], src_hi[:, 0:7, :, :])
+                    permute(by_column(b0[:, 992:1024]), src_hi[:, 7, 0:8, :])
+                    permute(by_column(b1[:, 0:32]), src_hi[:, 7, 8:16, :])
+                    permute(r1[:, :, 16:32, :], src_hi[:, 8:15, :, :])
+                    nc.vector.tensor_copy(out=mgr[:, g, 0:1024], in_=b0[:])
+                    nc.vector.tensor_copy(out=mgr[:, g, 1024:2048], in_=b1[:])
+                else:
+                    for s in range(15):
+                        d = s + 1
+                        src2 = mraw[:, g, :, 32 * d : 32 * d + 33 * 31 + 1 : 33].rearrange("q t a -> q a t")
+                        if s < 7:
+                            permute(r0[:, s, 0:N, :], src2)
+                        elif s == 7:
+                            permute(by_column(b0[:, 928:1024]), src2[:, 0:24, :])
+                            permute(by_column(b1[:, 0:32]), src2[:, 24:32, :])
+                        else:
+                            permute(r1[:, s - 8, 0:N, :], src2)
+                    nc.scalar.copy(out=mgr[:, 2 + g, 0:1024], in_=b0[:])
+                    nc.scalar.copy(out=mgr[:, 2 + g, 1024:2048], in_=b1[:])
+        for i in range(4):
+            nc.vector.quantize_mx(out=mcodes[:, i, :].bitcast(E4X4), scales=mscales[:, i, :], in_=mgr[:, i, :])
 
         def prepare_diagonal():
             for g in range(2):
@@ -276,6 +299,7 @@ def tile_tensorsquare_t_kernel(tc, features, mixing_matrix, grad_out, out):
         transposes(2, (0, 1))
         passes(0, 3)
         transposes(2, (2, 3))
+        periodic_features(1, nc.scalar.copy)
         plain_features(1, nc.scalar.copy)
         periodic_features(2, nc.scalar.copy)
         plain_features(2, nc.scalar.copy)
@@ -284,11 +308,9 @@ def tile_tensorsquare_t_kernel(tc, features, mixing_matrix, grad_out, out):
         quantise(1)
         products(0, 2)
         products(0, 3)
-        diag_product(0, slice(0, 1))
-        adds(nc.vector, 0, slice(0, 1))
         quantise(2)
-        diag_product(0, slice(1, U))
-        adds(nc.gpsimd, 0, slice(1, U))
+        diag_product(0)
+        adds(nc.gpsimd, 0, ALL)
         for n in range(1, LAST):
             more = n + 2 < GROUPS
             if n + 3 < GROUPS:
@@ -320,7 +342,7 @@ def tile_tensorsquare_t_kernel(tc, features, mixing_matrix, grad_out, out):
         diag_product(LAST)
         for u in range(1, U):
             products(LAST, u)
-        adds(nc.gpsimd, LAST, slice(0, 1))
+        adds(nc.gpsimd, LAST, slice(0, 2))
         finish(LAST - 1)
-        adds(nc.vector, LAST, slice(1, U))
+        adds(nc.vector, LAST, slice(2, U))
         finish(LAST)

@@ -18,6 +18,7 @@ Z, N, K = 4096, 32, 1024
 GROUPS = 8
 U = 4
 FLOPS = 2 * Z * K * N * N + 4 * Z * N * N
+SECOND = 544
 
 
 def tile_tensorsquare_t_kernel(tc, features, mixing_matrix, grad_out, out):
@@ -28,7 +29,6 @@ def tile_tensorsquare_t_kernel(tc, features, mixing_matrix, grad_out, out):
         graw_pool = ctx.enter_context(tc.tile_pool(name="graw", bufs=3))
         ggr_pool = ctx.enter_context(tc.tile_pool(name="ggr", bufs=2))
         gq_pool = ctx.enter_context(tc.tile_pool(name="gq", bufs=3))
-        fper_pool = ctx.enter_context(tc.tile_pool(name="fperp", bufs=3))
         small = ctx.enter_context(tc.tile_pool(name="small", bufs=2))
         ps_xt = ctx.enter_context(tc.psum_pool(name="psxt", bufs=2))
         ps_h = ctx.enter_context(tc.psum_pool(name="psh", bufs=4))
@@ -52,20 +52,12 @@ def tile_tensorsquare_t_kernel(tc, features, mixing_matrix, grad_out, out):
         o_view = out.rearrange("(g p u) c -> g p (u c)", g=GROUPS, p=P, u=U)
         m_view = mixing_matrix.rearrange("(g w q e) c -> g w q e c", g=2, w=2, q=P, e=2)
 
-        graws, ggrs, gqs, fpers, dsbs, dtps, pbs, r1s, s1s, s2s, hs = {}, {}, {}, {}, {}, {}, {}, {}, {}, {}, {}
+        graws, ggrs, gqs, dsbs, dtps, pbs, r1s, s1s, s2s, hs = {}, {}, {}, {}, {}, {}, {}, {}, {}, {}
 
         def load_group(n):
             graw = graw_pool.tile([P, U, K], BF16, name="graw")
             nc.sync.dma_start(out=graw[:].rearrange("p u k -> p (u k)"), in_=g_view[n])
             graws[n] = graw
-
-        def periodic_features(n, copy):
-            fper = fper_pool.tile([P, U, 16 * N], BF16, name="fper")
-            fpers[n] = fper
-            copy(
-                out=fper[:].bitcast(F32).rearrange("p u (r j) -> p u r j", j=N // 2),
-                in_=f_sb[:, n, :, :].bitcast(F32).unsqueeze(2).to_broadcast([P, U, 16, N // 2]),
-            )
 
         def plain_features(n, copy):
             copy(
@@ -83,7 +75,6 @@ def tile_tensorsquare_t_kernel(tc, features, mixing_matrix, grad_out, out):
                 nc.sync.dma_start(out=mraw[:, g, 2 * w : 2 * w + 2, 0:1024], in_=m_view[g, w])
         for n in range(3):
             load_group(n)
-        periodic_features(0, nc.vector.tensor_copy)
         m2_gu = m2[:].rearrange("p g u x -> p (g u) x")
         f_gu = f_sb[:].rearrange("p g u j -> p (g u) j")
         nc.scalar.copy(out=m2_gu[:, :, 0:496:33], in_=f_gu[:, :, 16:32])
@@ -219,7 +210,7 @@ def tile_tensorsquare_t_kernel(tc, features, mixing_matrix, grad_out, out):
 
         def diag_product(n, us=slice(0, U)):
             nc.vector.scalar_tensor_tensor(
-                out=pbs[n][:, us, 480:512], in0=dtps[n][:, us, 0:N], scalar=2.0, in1=f_sb[:, n, us, :], op0=MULT, op1=MULT
+                out=pbs[n][:, us, 496:528], in0=dtps[n][:, us, 0:N], scalar=2.0, in1=f_sb[:, n, us, :], op0=MULT, op1=MULT
             )
 
         def passes(n, u):
@@ -240,17 +231,17 @@ def tile_tensorsquare_t_kernel(tc, features, mixing_matrix, grad_out, out):
 
         def products(n, u):
             if n not in pbs:
-                pb_new = small.tile([P, U, 1024], F32, name="pb")
+                pb_new = small.tile([P, U, SECOND + 512], F32, name="pb")
                 pbs[n] = pb_new
             pb = pbs[n]
             h = hs[(n, u)]
             nc.vector.tensor_tensor(
-                out=pb[:, u, 0:480].rearrange("p (s a) -> p s a", a=N),
-                in0=h[:, 1:496].rearrange("p (s w) -> p s w", w=33)[:, :, 0:N],
-                in1=fpers[n][:, u, 1:496].rearrange("p (s w) -> p s w", w=33)[:, :, 0:N],
+                out=pb[:, u, 0:512].rearrange("p (r j) -> p r j", j=N),
+                in0=h[:].rearrange("p (r j) -> p r j", j=N),
+                in1=f_sb[:, n, u, :].unsqueeze(1).to_broadcast([P, 16, N]),
                 op=MULT,
             )
-            nc.vector.tensor_tensor(out=pb[:, u, 512:1024], in0=h[:], in1=m2[:, n, u, :], op=MULT)
+            nc.vector.tensor_tensor(out=pb[:, u, SECOND : SECOND + 512], in0=h[:], in1=m2[:, n, u, :], op=MULT)
 
         def adds(eng, n, us):
             if n not in s1s:
@@ -259,7 +250,12 @@ def tile_tensorsquare_t_kernel(tc, features, mixing_matrix, grad_out, out):
                 s2 = small.tile([P, 2, U, 128], F32, name="s2")
                 s2s[n] = s2
             pb = pbs[n]
-            eng.tensor_tensor(out=s1s[n][:, us, :], in0=pb[:, us, 0:512], in1=pb[:, us, 512:1024], op=ADD)
+            eng.tensor_tensor(
+                out=s1s[n][:, us, :].rearrange("p u (s a) -> p u s a", a=N),
+                in0=pb[:, us, 1:529].rearrange("p u (s w) -> p u s w", w=33)[:, :, :, 0:N],
+                in1=pb[:, us, SECOND : SECOND + 512].rearrange("p u (s a) -> p u s a", a=N),
+                op=ADD,
+            )
             eng.tensor_tensor(
                 out=s2s[n][:, :, us, :].rearrange("p g u x -> p u g x"),
                 in0=s1s[n][:, us, 0:256].rearrange("p u (g x) -> p u g x", g=2),
@@ -299,9 +295,7 @@ def tile_tensorsquare_t_kernel(tc, features, mixing_matrix, grad_out, out):
         transposes(2, (0, 1))
         passes(0, 3)
         transposes(2, (2, 3))
-        periodic_features(1, nc.scalar.copy)
         plain_features(1, nc.scalar.copy)
-        periodic_features(2, nc.scalar.copy)
         plain_features(2, nc.scalar.copy)
         products(0, 0)
         products(0, 1)
@@ -325,7 +319,6 @@ def tile_tensorsquare_t_kernel(tc, features, mixing_matrix, grad_out, out):
             diag_transposes(n)
             if more:
                 transposes(n + 2, (2, 3))
-                periodic_features(n + 2, nc.scalar.copy)
                 plain_features(n + 2, nc.scalar.copy)
             for u in range(U):
                 products(n, u)
@@ -339,10 +332,12 @@ def tile_tensorsquare_t_kernel(tc, features, mixing_matrix, grad_out, out):
             passes(LAST, u)
         diag_transposes(LAST)
         products(LAST, 0)
-        diag_product(LAST)
-        for u in range(1, U):
-            products(LAST, u)
+        products(LAST, 1)
+        diag_product(LAST, slice(0, 2))
         adds(nc.gpsimd, LAST, slice(0, 2))
+        products(LAST, 2)
+        products(LAST, 3)
+        diag_product(LAST, slice(2, U))
         finish(LAST - 1)
         adds(nc.vector, LAST, slice(2, U))
         finish(LAST)

@@ -18,6 +18,7 @@ Z, N, K = 4096, 32, 1024
 GROUPS = 8
 U = 4
 FLOPS = 2 * Z * K * N * N + 4 * Z * N * N
+V_SHARE = 4
 SECOND = 544
 
 
@@ -38,8 +39,6 @@ def tile_tensorsquare_t_kernel(tc, features, mixing_matrix, grad_out, out):
 
         ident = keep.tile([P, P], F32, name="ident")
         make_identity(nc, ident[:])
-        identb = keep.tile([P, P], BF16, name="identb")
-        make_identity(nc, identb[:])
         f_sb = keep.tile([P, GROUPS, U, N], BF16, name="f_sb")
         o_sb = keep.tile([P, GROUPS, U, N], F32, name="o_sb")
         mcodes = keep.tile([P, 4, 512], U32, name="mcodes", align_bytes=64)
@@ -77,66 +76,48 @@ def tile_tensorsquare_t_kernel(tc, features, mixing_matrix, grad_out, out):
             load_group(n)
         m2_gu = m2[:].rearrange("p g u x -> p (g u) x")
         f_gu = f_sb[:].rearrange("p g u j -> p (g u) j")
-        nc.scalar.copy(out=m2_gu[:, :, 0:496:33], in_=f_gu[:, :, 16:32])
-        nc.scalar.copy(out=m2_gu[:, :, 496:512], in_=f_gu[:, :, 0:16])
-        plain_features(0, nc.scalar.copy)
+
+        def single_features(gus, copy):
+            copy(out=m2_gu[:, gus, 0:496:33], in_=f_gu[:, gus, 16:32])
+            copy(out=m2_gu[:, gus, 496:512], in_=f_gu[:, gus, 0:16])
+
+        single_features(slice(0, 3 * U), nc.vector.tensor_copy)
+        plain_features(0, nc.vector.tensor_copy)
+        single_features(slice(3 * U, GROUPS * U), nc.scalar.copy)
 
         msw = mprep.tile([P, 2, 4, 544], BF16, name="msw")
         mgr = mprep.tile([P, 4, 512 * 4], BF16, name="mgr", align_bytes=64)
         mgd = mprep.tile([P, 2, P * 4], BF16, name="mgd", align_bytes=64)
         nc.gpsimd.memset(mgd[:], 0.0)
-
-        def permute(dst, src):
-            nc.tensor.matmul(out=dst, lhsT=identb[:], rhs=src, start=True, stop=True)
-
-        def by_column(ap):
-            return ap.rearrange("q (a t) -> q a t", t=4)
-
         for g in range(2):
             nc.vector.tensor_copy(out=mraw[:, g, :, 1024:1536], in_=mraw[:, g, :, 0:512])
+            run_lo = mraw[:, g, :, 16 : 16 + 33 * 15 + 1 : 33].rearrange("q t a -> q a t")
+            run_hi = mraw[:, g, :, 512 : 512 + 33 * 15 + 1 : 33].rearrange("q t a -> q a t")
+            cols1 = mgr[:, g, :].rearrange("q (x t) -> q x t", t=4)
+            cols2 = mgr[:, 2 + g, :].rearrange("q (x t) -> q x t", t=4)
+            nc.scalar.copy(out=cols1[:, 0:496:33, :], in_=run_lo)
+            nc.scalar.copy(out=cols1[:, 496:512, :], in_=run_hi)
+            dst2 = mgr[:, 2 + g, 4:1984].rearrange("q (s w t) -> q s w t", w=33, t=4)
+            for d in range(1, 16):
+                src2 = mraw[:, g, :, 32 * d : 32 * d + 33 * 31 + 1 : 33].rearrange("q t a -> q a t")
+                if d <= V_SHARE:
+                    nc.vector.tensor_copy(out=dst2[:, d - 1, 0:N, :], in_=src2)
+                else:
+                    nc.scalar.copy(out=dst2[:, d - 1, 0:N, :], in_=src2)
+            nc.scalar.copy(out=cols2[:, 0:496:33, :], in_=run_hi)
+            nc.scalar.copy(out=cols2[:, 496:512, :], in_=run_lo)
             rows_hi = mraw[:, g, :, 512:1024].rearrange("q t (a h x) -> q t a h x", h=2, x=16)
             sw = msw[:, g, :, 0:512].rearrange("q t (a h x) -> q t a h x", h=2, x=16)
             nc.vector.tensor_copy(out=sw[:, :, :, 0, :], in_=rows_hi[:, :, :, 1, :])
             nc.vector.tensor_copy(out=sw[:, :, :, 1, :], in_=rows_hi[:, :, :, 0, :])
-        for g in range(2):
-            run_lo = mraw[:, g, :, 16 : 16 + 33 * 15 + 1 : 33].rearrange("q t a -> q a t")
-            run_hi = mraw[:, g, :, 512 : 512 + 33 * 15 + 1 : 33].rearrange("q t a -> q a t")
+            dst = mgr[:, g, 4:1984].rearrange("q (s w t) -> q s w t", w=33, t=4)
             src_lo = mraw[:, g, :, 1 : 1 + 33 * 16].rearrange("q t (a w) -> q w a t", w=33)
+            nc.vector.tensor_copy(out=dst[:, :, 0:16, :], in_=src_lo[:, 0:15, :, :])
             src_hi = msw[:, g, :, 1 : 1 + 33 * 16].rearrange("q t (a w) -> q w a t", w=33)
-            for source in range(2):
-                b0 = ps_h.tile([P, 1024], BF16, name="h")
-                b1 = ps_h.tile([P, 1024], BF16, name="h")
-                r0 = b0[:, 4:928].rearrange("q (s w t) -> q s w t", w=33, t=4)
-                r1 = b1[:, 36:960].rearrange("q (s w t) -> q s w t", w=33, t=4)
-                first, second = (run_lo, run_hi) if source == 0 else (run_hi, run_lo)
-                permute(by_column(b0[:])[:, 0:232:33, :], first[:, 0:8, :])
-                permute(by_column(b1[:])[:, 8:240:33, :], first[:, 8:16, :])
-                permute(by_column(b1[:, 960:1024]), second)
-                if source == 0:
-                    permute(r0[:, :, 0:16, :], src_lo[:, 0:7, :, :])
-                    permute(by_column(b0[:, 928:992]), src_lo[:, 7, :, :])
-                    permute(r1[:, :, 0:16, :], src_lo[:, 8:15, :, :])
-                    permute(r0[:, :, 16:32, :], src_hi[:, 0:7, :, :])
-                    permute(by_column(b0[:, 992:1024]), src_hi[:, 7, 0:8, :])
-                    permute(by_column(b1[:, 0:32]), src_hi[:, 7, 8:16, :])
-                    permute(r1[:, :, 16:32, :], src_hi[:, 8:15, :, :])
-                    nc.vector.tensor_copy(out=mgr[:, g, 0:1024], in_=b0[:])
-                    nc.vector.tensor_copy(out=mgr[:, g, 1024:2048], in_=b1[:])
-                else:
-                    for s in range(15):
-                        d = s + 1
-                        src2 = mraw[:, g, :, 32 * d : 32 * d + 33 * 31 + 1 : 33].rearrange("q t a -> q a t")
-                        if s < 7:
-                            permute(r0[:, s, 0:N, :], src2)
-                        elif s == 7:
-                            permute(by_column(b0[:, 928:1024]), src2[:, 0:24, :])
-                            permute(by_column(b1[:, 0:32]), src2[:, 24:32, :])
-                        else:
-                            permute(r1[:, s - 8, 0:N, :], src2)
-                    nc.scalar.copy(out=mgr[:, 2 + g, 0:1024], in_=b0[:])
-                    nc.scalar.copy(out=mgr[:, 2 + g, 1024:2048], in_=b1[:])
-        for i in range(4):
-            nc.vector.quantize_mx(out=mcodes[:, i, :].bitcast(E4X4), scales=mscales[:, i, :], in_=mgr[:, i, :])
+            nc.vector.tensor_copy(out=dst[:, :, 16:32, :], in_=src_hi[:, 0:15, :, :])
+            nc.vector.quantize_mx(out=mcodes[:, g, :].bitcast(E4X4), scales=mscales[:, g, :], in_=mgr[:, g, :])
+        nc.vector.quantize_mx(out=mcodes[:, 2, :].bitcast(E4X4), scales=mscales[:, 2, :], in_=mgr[:, 2, :])
+        nc.vector.quantize_mx(out=mcodes[:, 3, :].bitcast(E4X4), scales=mscales[:, 3, :], in_=mgr[:, 3, :])
 
         def prepare_diagonal():
             for g in range(2):
@@ -283,6 +264,7 @@ def tile_tensorsquare_t_kernel(tc, features, mixing_matrix, grad_out, out):
         new_codes(0)
         for u in range(U):
             quantise_tile(0, u)
+        plain_features(1, nc.vector.tensor_copy)
         prepare_diagonal()
         passes(0, 0)
         transposes(1, (0, 1))
@@ -295,16 +277,17 @@ def tile_tensorsquare_t_kernel(tc, features, mixing_matrix, grad_out, out):
         transposes(2, (0, 1))
         passes(0, 3)
         transposes(2, (2, 3))
-        plain_features(1, nc.scalar.copy)
-        plain_features(2, nc.scalar.copy)
         products(0, 0)
         products(0, 1)
+        plain_features(2, nc.vector.tensor_copy)
         quantise(1)
         products(0, 2)
         products(0, 3)
+        diag_product(0, slice(0, 1))
+        adds(nc.vector, 0, slice(0, 1))
         quantise(2)
-        diag_product(0)
-        adds(nc.gpsimd, 0, ALL)
+        diag_product(0, slice(1, U))
+        adds(nc.gpsimd, 0, slice(1, U))
         for n in range(1, LAST):
             more = n + 2 < GROUPS
             if n + 3 < GROUPS:
@@ -332,12 +315,11 @@ def tile_tensorsquare_t_kernel(tc, features, mixing_matrix, grad_out, out):
             passes(LAST, u)
         diag_transposes(LAST)
         products(LAST, 0)
-        products(LAST, 1)
-        diag_product(LAST, slice(0, 2))
-        adds(nc.gpsimd, LAST, slice(0, 2))
-        products(LAST, 2)
-        products(LAST, 3)
-        diag_product(LAST, slice(2, U))
+        diag_product(LAST, slice(0, 1))
+        adds(nc.gpsimd, LAST, slice(0, 1))
+        for u in range(1, U):
+            products(LAST, u)
+        diag_product(LAST, slice(1, U))
         finish(LAST - 1)
-        adds(nc.vector, LAST, slice(2, U))
+        adds(nc.vector, LAST, slice(1, U))
         finish(LAST)

@@ -226,8 +226,10 @@ def tile_tensorsquare_t_kernel(tc, features, mixing_matrix, grad_out, out):
 
         def adds(eng, n, us):
             if n not in s1s:
-                s1 = small.tile([P, U, 512], F32, name="s1")
-                s1s[n] = s1
+                if n + 2 not in ggrs:
+                    ggr_free = ggr_pool.tile([P, 2 * U * P * 4], BF16, name="ggr", align_bytes=64)
+                    ggrs[n + 2] = ggr_free
+                s1s[n] = ggrs[n + 2][:].bitcast(F32).rearrange("p (u x) -> p u x", u=U)
                 s2 = small.tile([P, 2, U, 128], F32, name="s2")
                 s2s[n] = s2
             pb = pbs[n]
@@ -283,11 +285,9 @@ def tile_tensorsquare_t_kernel(tc, features, mixing_matrix, grad_out, out):
         quantise(1)
         products(0, 2)
         products(0, 3)
-        diag_product(0, slice(0, 1))
-        adds(nc.vector, 0, slice(0, 1))
+        diag_product(0)
         quantise(2)
-        diag_product(0, slice(1, U))
-        adds(nc.gpsimd, 0, slice(1, U))
+        adds(nc.gpsimd, 0, ALL)
         for n in range(1, LAST):
             more = n + 2 < GROUPS
             if n + 3 < GROUPS:
@@ -305,9 +305,9 @@ def tile_tensorsquare_t_kernel(tc, features, mixing_matrix, grad_out, out):
                 plain_features(n + 2, nc.scalar.copy)
             for u in range(U):
                 products(n, u)
+            diag_product(n)
             if more:
                 quantise(n + 2)
-            diag_product(n)
             adds(nc.gpsimd, n, ALL)
             finish(n - 1)
         diag_passes(LAST)

@@ -19,6 +19,7 @@ GROUPS = 8
 U = 4
 FLOPS = 2 * Z * K * N * N + 4 * Z * N * N
 V_SHARE = 4
+G_TILES = 3
 SECOND = 544
 
 
@@ -224,13 +225,13 @@ def tile_tensorsquare_t_kernel(tc, features, mixing_matrix, grad_out, out):
             )
             nc.vector.tensor_tensor(out=pb[:, u, SECOND : SECOND + 512], in0=h[:], in1=m2[:, n, u, :], op=MULT)
 
-        def adds(eng, n, us):
+        def first_adds(eng, n, us):
             if n not in s1s:
                 if n + 2 not in ggrs:
                     ggr_free = ggr_pool.tile([P, 2 * U * P * 4], BF16, name="ggr", align_bytes=64)
                     ggrs[n + 2] = ggr_free
                 s1s[n] = ggrs[n + 2][:].bitcast(F32).rearrange("p (u x) -> p u x", u=U)
-                s2 = small.tile([P, 2, U, 128], F32, name="s2")
+                s2 = small.tile([P, U, 256], F32, name="s2")
                 s2s[n] = s2
             pb = pbs[n]
             eng.tensor_tensor(
@@ -239,22 +240,40 @@ def tile_tensorsquare_t_kernel(tc, features, mixing_matrix, grad_out, out):
                 in1=pb[:, us, SECOND : SECOND + 512].rearrange("p u (s a) -> p u s a", a=N),
                 op=ADD,
             )
-            eng.tensor_tensor(
-                out=s2s[n][:, :, us, :].rearrange("p g u x -> p u g x"),
-                in0=s1s[n][:, us, 0:256].rearrange("p u (g x) -> p u g x", g=2),
-                in1=s1s[n][:, us, 256:512].rearrange("p u (g x) -> p u g x", g=2),
-                op=ADD,
-            )
 
-        def finish(n):
-            r1 = small.tile([P, 2, U, N], F32, name="r1")
+        def second_adds(eng, n, us):
+            eng.tensor_tensor(out=s2s[n][:, us, :], in0=s1s[n][:, us, 0:256], in1=s1s[n][:, us, 256:512], op=ADD)
+
+        def adds(eng, n, us):
+            first_adds(eng, n, us)
+            second_adds(eng, n, us)
+
+        def finish(n, k):
+            r1 = small.tile([P, 2 * U, N], F32, name="r1")
             nc.vector.tensor_reduce(
-                out=r1[:].rearrange("p g u c -> p (g u) c"),
-                in_=s2s[n][:].rearrange("p g u (r c) -> p (g u) c r", c=N),
+                out=r1[:, 0 : 2 * k, :],
+                in_=s2s[n][:, 0:k, :].rearrange("p u (g r c) -> p (u g) c r", r=4, c=N),
                 axis=AX,
                 op=ADD,
             )
-            nc.vector.tensor_reduce(out=o_sb[:, n, :, :], in_=r1[:].rearrange("p r u c -> p u c r"), axis=AX, op=ADD)
+            if k < U:
+                r1b = small.tile([P, 4 * U, N], F32, name="r1b")
+                nc.vector.tensor_reduce(
+                    out=r1b[:, 0 : 4 * (U - k), :],
+                    in_=s1s[n][:, k:U, :].rearrange("p u (q r c) -> p (u q) c r", r=4, c=N),
+                    axis=AX,
+                    op=ADD,
+                )
+            nc.vector.tensor_reduce(
+                out=o_sb[:, n, 0:k, :], in_=r1[:, 0 : 2 * k, :].rearrange("p (u g) c -> p u c g", g=2), axis=AX, op=ADD
+            )
+            if k < U:
+                nc.vector.tensor_reduce(
+                    out=o_sb[:, n, k:U, :],
+                    in_=r1b[:, 0 : 4 * (U - k), :].rearrange("p (u q) c -> p u c q", q=4),
+                    axis=AX,
+                    op=ADD,
+                )
             first_store = GROUPS - 4
             if n >= first_store:
                 for m in range(0 if n == first_store else n, n + 1):
@@ -287,7 +306,8 @@ def tile_tensorsquare_t_kernel(tc, features, mixing_matrix, grad_out, out):
         products(0, 3)
         diag_product(0)
         quantise(2)
-        adds(nc.gpsimd, 0, ALL)
+        first_adds(nc.gpsimd, 0, ALL)
+        second_adds(nc.gpsimd, 0, slice(0, G_TILES))
         for n in range(1, LAST):
             more = n + 2 < GROUPS
             if n + 3 < GROUPS:
@@ -308,8 +328,9 @@ def tile_tensorsquare_t_kernel(tc, features, mixing_matrix, grad_out, out):
             diag_product(n)
             if more:
                 quantise(n + 2)
-            adds(nc.gpsimd, n, ALL)
-            finish(n - 1)
+            first_adds(nc.gpsimd, n, ALL)
+            second_adds(nc.gpsimd, n, slice(0, G_TILES))
+            finish(n - 1, G_TILES)
         diag_passes(LAST)
         for u in range(U):
             passes(LAST, u)
@@ -320,6 +341,6 @@ def tile_tensorsquare_t_kernel(tc, features, mixing_matrix, grad_out, out):
         for u in range(1, U):
             products(LAST, u)
         diag_product(LAST, slice(1, U))
-        finish(LAST - 1)
+        finish(LAST - 1, G_TILES)
         adds(nc.vector, LAST, slice(1, U))
-        finish(LAST)
+        finish(LAST, U)

@@ -82,9 +82,9 @@ def tile_tensorsquare_t_kernel(tc, features, mixing_matrix, grad_out, out):
             copy(out=m2_gu[:, gus, 0:496:33], in_=f_gu[:, gus, 16:32])
             copy(out=m2_gu[:, gus, 496:512], in_=f_gu[:, gus, 0:16])
 
-        single_features(slice(0, 3 * U), nc.vector.tensor_copy)
+        single_features(slice(0, U), nc.vector.tensor_copy)
         plain_features(0, nc.vector.tensor_copy)
-        single_features(slice(3 * U, GROUPS * U), nc.scalar.copy)
+        single_features(slice(U, GROUPS * U), nc.scalar.copy)
 
         msw = mprep.tile([P, 2, 4, 544], BF16, name="msw")
         mgr = mprep.tile([P, 4, 512 * 4], BF16, name="mgr", align_bytes=64)
@@ -282,10 +282,10 @@ def tile_tensorsquare_t_kernel(tc, features, mixing_matrix, grad_out, out):
         LAST = GROUPS - 1
         ALL = slice(0, U)
         transposes(0, (0, 1, 2, 3))
+        plain_features(1, nc.scalar.copy)
         new_codes(0)
         for u in range(U):
             quantise_tile(0, u)
-        plain_features(1, nc.vector.tensor_copy)
         prepare_diagonal()
         passes(0, 0)
         transposes(1, (0, 1))
@@ -298,9 +298,9 @@ def tile_tensorsquare_t_kernel(tc, features, mixing_matrix, grad_out, out):
         transposes(2, (0, 1))
         passes(0, 3)
         transposes(2, (2, 3))
+        plain_features(2, nc.scalar.copy)
         products(0, 0)
         products(0, 1)
-        plain_features(2, nc.vector.tensor_copy)
         quantise(1)
         products(0, 2)
         products(0, 3)

@@ -18,7 +18,7 @@ Z, N, K = 4096, 32, 1024
 GROUPS = 8
 U = 4
 FLOPS = 2 * Z * K * N * N + 4 * Z * N * N
-V_SHARE = 4
+V_SHARE = 8
 G_TILES = 3
 SECOND = 544
 
@@ -132,13 +132,18 @@ def tile_tensorsquare_t_kernel(tc, features, mixing_matrix, grad_out, out):
                 in_=mgd[:].rearrange("q g s -> q (g s)"),
             )
 
-        def transposes(n, us):
+        def transposes(n, us, spare_banks=False):
             if n not in ggrs:
                 ggr_new = ggr_pool.tile([P, 2 * U * P * 4], BF16, name="ggr", align_bytes=64)
                 ggrs[n] = ggr_new
             ggr_w = ggrs[n][:].bitcast(F32).rearrange("q (g u z w) -> q g u z w", g=2, u=U, z=P, w=2)
             for u in us:
-                xt = ps_xt.tile([P, 4, P], F32, name="xt")
+                if not spare_banks:
+                    xt = ps_xt.tile([P, 4, P], F32, name="xt")
+                elif u % 2 == 0:
+                    xt = ps_d.tile([P, 4, P], F32, name="accd")
+                else:
+                    xt = ps_dt.tile([P, 4, P], F32, name="dtp")
                 words = graws[n][:, u, :].bitcast(F32)
                 for b in range(4):
                     nc.tensor.transpose(xt[:, b, :], words[:, b * P : (b + 1) * P], ident[:])
@@ -282,21 +287,21 @@ def tile_tensorsquare_t_kernel(tc, features, mixing_matrix, grad_out, out):
         LAST = GROUPS - 1
         ALL = slice(0, U)
         transposes(0, (0, 1, 2, 3))
-        plain_features(1, nc.scalar.copy)
         new_codes(0)
         for u in range(U):
             quantise_tile(0, u)
         prepare_diagonal()
+        transposes(1, (0, 1), spare_banks=True)
+        transposes(1, (2, 3))
+        plain_features(1, nc.scalar.copy)
         passes(0, 0)
-        transposes(1, (0, 1))
         passes(0, 1)
         diag_passes(0)
-        transposes(1, (2, 3))
+        transposes(2, (0, 1))
         passes(0, 2)
         load_group(3)
-        diag_transposes(0)
-        transposes(2, (0, 1))
         passes(0, 3)
+        diag_transposes(0)
         transposes(2, (2, 3))
         plain_features(2, nc.scalar.copy)
         products(0, 0)

from contextlib import ExitStack

import concourse.mybir as mybir
from concourse.masks import make_identity

F32 = mybir.dt.float32
BF16 = mybir.dt.bfloat16
U32 = mybir.dt.uint32
U8 = mybir.dt.uint8
E4X4 = mybir.dt.float8_e4m3fn_x4
E5X4 = mybir.dt.float8_e5m2_x4
MULT = mybir.AluOpType.mult
ADD = mybir.AluOpType.add
AX = mybir.AxisListType.X

P = 128
Z, N, K = 4096, 32, 1024
GROUPS = 8
U = 4
FLOPS = 2 * Z * K * N * N + 4 * Z * N * N
V_SHARE = 8
G_TILES = 3
SECOND = 544


def tile_tensorsquare_t_kernel(tc, features, mixing_matrix, grad_out, out):
    nc = tc.nc
    with ExitStack() as ctx:
        keep = ctx.enter_context(tc.tile_pool(name="keep", bufs=1))
        mprep = ctx.enter_context(tc.tile_pool(name="mprep", bufs=1))
        graw_pool = ctx.enter_context(tc.tile_pool(name="graw", bufs=3))
        ggr_pool = ctx.enter_context(tc.tile_pool(name="ggr", bufs=2))
        gq_pool = ctx.enter_context(tc.tile_pool(name="gq", bufs=3))
        small = ctx.enter_context(tc.tile_pool(name="small", bufs=2))
        ps_xt = ctx.enter_context(tc.psum_pool(name="psxt", bufs=2))
        ps_h = ctx.enter_context(tc.psum_pool(name="psh", bufs=4))
        ps_d = ctx.enter_context(tc.psum_pool(name="psd", bufs=1))
        ps_dt = ctx.enter_context(tc.psum_pool(name="psdt", bufs=1))
        ctx.enter_context(tc.manual_schedule())

        ident = keep.tile([P, P], F32, name="ident")
        make_identity(nc, ident[:])
        f_sb = keep.tile([P, GROUPS, U, N], BF16, name="f_sb")
        o_sb = keep.tile([P, GROUPS, U, N], F32, name="o_sb")
        mcodes = keep.tile([P, 4, 512], U32, name="mcodes", align_bytes=64)
        mscales = keep.tile([P, 4, 512], U8, name="mscales", align_bytes=64)
        dcodes = keep.tile([P, 2, P], U32, name="dcodes", align_bytes=64)
        dscales = keep.tile([P, 2, P], U8, name="dscales", align_bytes=64)
        m2 = keep.tile([P, GROUPS, U, 512], BF16, name="m2")

        g_view = grad_out.rearrange("(g p u) k -> g p (u k)", g=GROUPS, p=P, u=U)
        o_view = out.rearrange("(g p u) c -> g p (u c)", g=GROUPS, p=P, u=U)
        m_view = mixing_matrix.rearrange("(g w q e) c -> g w q e c", g=2, w=2, q=P, e=2)

        graws, ggrs, gqs, dsbs, dtps, pbs, r1s, s1s, s2s, hs = {}, {}, {}, {}, {}, {}, {}, {}, {}, {}

        def load_group(n):
            graw = graw_pool.tile([P, U, K], BF16, name="graw")
            nc.sync.dma_start(out=graw[:].rearrange("p u k -> p (u k)"), in_=g_view[n])
            graws[n] = graw

        def plain_features(n, copy):
            copy(
                out=m2[:, n, :, 0:495].rearrange("p u (s w) -> p u s w", w=33)[:, :, :, 1:33],
                in_=f_sb[:, n, :, :].unsqueeze(2).to_broadcast([P, U, 15, N]),
            )

        nc.scalar.dma_start(
            out=f_sb[:].rearrange("p g u j -> p g (u j)"),
            in_=features.rearrange("(g p u) j -> p g (u j)", g=GROUPS, p=P, u=U),
        )
        mraw = mprep.tile([P, 2, 4, 1536], BF16, name="mraw")
        for g in range(2):
            for w in range(2):
                nc.sync.dma_start(out=mraw[:, g, 2 * w : 2 * w + 2, 0:1024], in_=m_view[g, w])
        for n in range(3):
            load_group(n)
        m2_gu = m2[:].rearrange("p g u x -> p (g u) x")
        f_gu = f_sb[:].rearrange("p g u j -> p (g u) j")

        def single_features(gus, copy):
            copy(out=m2_gu[:, gus, 0:496:33], in_=f_gu[:, gus, 16:32])
            copy(out=m2_gu[:, gus, 496:512], in_=f_gu[:, gus, 0:16])

        single_features(slice(0, U), nc.vector.tensor_copy)
        plain_features(0, nc.vector.tensor_copy)
        single_features(slice(U, GROUPS * U), nc.scalar.copy)

        msw = mprep.tile([P, 2, 4, 544], BF16, name="msw")
        mgr = mprep.tile([P, 4, 512 * 4], BF16, name="mgr", align_bytes=64)
        mgd = mprep.tile([P, 2, P * 4], BF16, name="mgd", align_bytes=64)
        nc.gpsimd.memset(mgd[:], 0.0)
        for g in range(2):
            nc.vector.tensor_copy(out=mraw[:, g, :, 1024:1536], in_=mraw[:, g, :, 0:512])
            run_lo = mraw[:, g, :, 16 : 16 + 33 * 15 + 1 : 33].rearrange("q t a -> q a t")
            run_hi = mraw[:, g, :, 512 : 512 + 33 * 15 + 1 : 33].rearrange("q t a -> q a t")
            cols1 = mgr[:, g, :].rearrange("q (x t) -> q x t", t=4)
            cols2 = mgr[:, 2 + g, :].rearrange("q (x t) -> q x t", t=4)
            nc.scalar.copy(out=cols1[:, 0:496:33, :], in_=run_lo)
            nc.scalar.copy(out=cols1[:, 496:512, :], in_=run_hi)
            dst2 = mgr[:, 2 + g, 4:1984].rearrange("q (s w t) -> q s w t", w=33, t=4)
            for d in range(1, 16):
                src2 = mraw[:, g, :, 32 * d : 32 * d + 33 * 31 + 1 : 33].rearrange("q t a -> q a t")
                if d <= V_SHARE:
                    nc.vector.tensor_copy(out=dst2[:, d - 1, 0:N, :], in_=src2)
                else:
                    nc.scalar.copy(out=dst2[:, d - 1, 0:N, :], in_=src2)
            nc.scalar.copy(out=cols2[:, 0:496:33, :], in_=run_hi)
            nc.scalar.copy(out=cols2[:, 496:512, :], in_=run_lo)
            rows_hi = mraw[:, g, :, 512:1024].rearrange("q t (a h x) -> q t a h x", h=2, x=16)
            sw = msw[:, g, :, 0:512].rearrange("q t (a h x) -> q t a h x", h=2, x=16)
            nc.vector.tensor_copy(out=sw[:, :, :, 0, :], in_=rows_hi[:, :, :, 1, :])
            nc.vector.tensor_copy(out=sw[:, :, :, 1, :], in_=rows_hi[:, :, :, 0, :])
            dst = mgr[:, g, 4:1984].rearrange("q (s w t) -> q s w t", w=33, t=4)
            src_lo = mraw[:, g, :, 1 : 1 + 33 * 16].rearrange("q t (a w) -> q w a t", w=33)
            nc.vector.tensor_copy(out=dst[:, :, 0:16, :], in_=src_lo[:, 0:15, :, :])
            src_hi = msw[:, g, :, 1 : 1 + 33 * 16].rearrange("q t (a w) -> q w a t", w=33)
            nc.vector.tensor_copy(out=dst[:, :, 16:32, :], in_=src_hi[:, 0:15, :, :])
            nc.vector.quantize_mx(out=mcodes[:, g, :].bitcast(E4X4), scales=mscales[:, g, :], in_=mgr[:, g, :])
        nc.vector.quantize_mx(out=mcodes[:, 2, :].bitcast(E4X4), scales=mscales[:, 2, :], in_=mgr[:, 2, :])
        nc.vector.quantize_mx(out=mcodes[:, 3, :].bitcast(E4X4), scales=mscales[:, 3, :], in_=mgr[:, 3, :])

        def prepare_diagonal():
            for g in range(2):
                nc.vector.tensor_copy(
                    out=mgd[:, g, 0 : N * 4].rearrange("q (a t) -> q a t", t=4),
                    in_=mraw[:, g, :, 0 : 33 * 31 + 1 : 33].rearrange("q t a -> q a t"),
                )
            nc.vector.quantize_mx(
                out=dcodes[:].rearrange("q g s -> q (g s)").bitcast(E4X4),
                scales=dscales[:].rearrange("q g s -> q (g s)"),
                in_=mgd[:].rearrange("q g s -> q (g s)"),
            )

        def transposes(n, us, spare_banks=False):
            if n not in ggrs:
                ggr_new = ggr_pool.tile([P, 2 * U * P * 4], BF16, name="ggr", align_bytes=64)
                ggrs[n] = ggr_new
            ggr_w = ggrs[n][:].bitcast(F32).rearrange("q (g u z w) -> q g u z w", g=2, u=U, z=P, w=2)
            for u in us:
                if not spare_banks:
                    xt = ps_xt.tile([P, 4, P], F32, name="xt")
                elif u % 2 == 0:
                    xt = ps_d.tile([P, 4, P], F32, name="accd")
                else:
                    xt = ps_dt.tile([P, 4, P], F32, name="dtp")
                words = graws[n][:, u, :].bitcast(F32)
                for b in range(4):
                    nc.tensor.transpose(xt[:, b, :], words[:, b * P : (b + 1) * P], ident[:])
                nc.scalar.copy(out=ggr_w[:, :, u, :, :], in_=xt[:].rearrange("q (g w) z -> q g z w", w=2))

        def new_codes(n):
            gcodes = gq_pool.tile([P, 2, 512], U32, name="gcodes", align_bytes=64)
            gscales = gq_pool.tile([P, 2, 512], U8, name="gscales", align_bytes=64)
            gqs[n] = (gcodes, gscales)

        def quantise_tile(n, u):
            gcodes, gscales = gqs[n]
            for g in range(2):
                nc.vector.quantize_mx(
                    out=gcodes[:, g, u * P : (u + 1) * P].bitcast(E5X4),
                    scales=gscales[:, g, u * P : (u + 1) * P],
                    in_=ggrs[n][:, g * 2048 + u * 512 : g * 2048 + (u + 1) * 512],
                )

        def quantise(n):
            new_codes(n)
            gcodes, gscales = gqs[n]
            nc.vector.quantize_mx(
                out=gcodes[:].rearrange("q g s -> q (g s)").bitcast(E5X4),
                scales=gscales[:].rearrange("q g s -> q (g s)"),
                in_=ggrs[n][:],
            )

        def diag_passes(n):
            gcodes, gscales = gqs[n]
            accd = ps_d.tile([P, 512], F32, name="accd")
            for g in range(2):
                nc.tensor.matmul_mx(
                    out=accd[:],
                    lhsT=dcodes[:, g, :].bitcast(E4X4),
                    lhsT_scale=dscales[:, g, :],
                    rhs=gcodes[:, g, :].bitcast(E5X4),
                    rhs_scale=gscales[:, g, :],
                    start=(g == 0),
                    stop=(g == 1),
                )
            dsb = small.tile([P, 512], F32, name="dsb")
            dsbs[n] = dsb
            nc.scalar.copy(out=dsb[:], in_=accd[:])

        def diag_transposes(n):
            dtp = ps_dt.tile([P, U, P], F32, name="dtp")
            dtps[n] = dtp
            for u in range(U):
                nc.tensor.transpose(dtp[:, u, :], dsbs[n][:, u * P : (u + 1) * P], ident[:])

        def diag_product(n, us=slice(0, U)):
            nc.vector.scalar_tensor_tensor(
                out=pbs[n][:, us, 496:528], in0=dtps[n][:, us, 0:N], scalar=2.0, in1=f_sb[:, n, us, :], op0=MULT, op1=MULT
            )

        def passes(n, u):
            gcodes, gscales = gqs[n]
            h = ps_h.tile([P, 512], F32, name="h")
            hs[(n, u)] = h
            cols = slice(u * P, (u + 1) * P)
            for i, (g, s) in enumerate(((0, 0), (0, 2), (1, 1), (1, 3))):
                nc.tensor.matmul_mx(
                    out=h[:],
                    lhsT=gcodes[:, g, cols].bitcast(E5X4),
                    lhsT_scale=gscales[:, g, cols],
                    rhs=mcodes[:, s, :].bitcast(E4X4),
                    rhs_scale=mscales[:, s, :],
                    start=(i == 0),
                    stop=(i == 3),
                )

        def products(n, u):
            if n not in pbs:
                pb_new = small.tile([P, U, SECOND + 512], F32, name="pb")
                pbs[n] = pb_new
            pb = pbs[n]
            h = hs[(n, u)]
            nc.vector.tensor_tensor(
                out=pb[:, u, 0:512].rearrange("p (r j) -> p r j", j=N),
                in0=h[:].rearrange("p (r j) -> p r j", j=N),
                in1=f_sb[:, n, u, :].unsqueeze(1).to_broadcast([P, 16, N]),
                op=MULT,
            )
            nc.vector.tensor_tensor(out=pb[:, u, SECOND : SECOND + 512], in0=h[:], in1=m2[:, n, u, :], op=MULT)

        def first_adds(eng, n, us):
            if n not in s1s:
                if n + 2 not in ggrs:
                    ggr_free = ggr_pool.tile([P, 2 * U * P * 4], BF16, name="ggr", align_bytes=64)
                    ggrs[n + 2] = ggr_free
                s1s[n] = ggrs[n + 2][:].bitcast(F32).rearrange("p (u x) -> p u x", u=U)
                s2 = small.tile([P, U, 256], F32, name="s2")
                s2s[n] = s2
            pb = pbs[n]
            eng.tensor_tensor(
                out=s1s[n][:, us, :].rearrange("p u (s a) -> p u s a", a=N),
                in0=pb[:, us, 1:529].rearrange("p u (s w) -> p u s w", w=33)[:, :, :, 0:N],
                in1=pb[:, us, SECOND : SECOND + 512].rearrange("p u (s a) -> p u s a", a=N),
                op=ADD,
            )

        def second_adds(eng, n, us):
            eng.tensor_tensor(out=s2s[n][:, us, :], in0=s1s[n][:, us, 0:256], in1=s1s[n][:, us, 256:512], op=ADD)

        def adds(eng, n, us):
            first_adds(eng, n, us)
            second_adds(eng, n, us)

        def finish(n, k):
            r1 = small.tile([P, 2 * U, N], F32, name="r1")
            nc.vector.tensor_reduce(
                out=r1[:, 0 : 2 * k, :],
                in_=s2s[n][:, 0:k, :].rearrange("p u (g r c) -> p (u g) c r", r=4, c=N),
                axis=AX,
                op=ADD,
            )
            if k < U:
                r1b = small.tile([P, 4 * U, N], F32, name="r1b")
                nc.vector.tensor_reduce(
                    out=r1b[:, 0 : 4 * (U - k), :],
                    in_=s1s[n][:, k:U, :].rearrange("p u (q r c) -> p (u q) c r", r=4, c=N),
                    axis=AX,
                    op=ADD,
                )
            nc.vector.tensor_reduce(
                out=o_sb[:, n, 0:k, :], in_=r1[:, 0 : 2 * k, :].rearrange("p (u g) c -> p u c g", g=2), axis=AX, op=ADD
            )
            if k < U:
                nc.vector.tensor_reduce(
                    out=o_sb[:, n, k:U, :],
                    in_=r1b[:, 0 : 4 * (U - k), :].rearrange("p (u q) c -> p u c q", q=4),
                    axis=AX,
                    op=ADD,
                )
            first_store = GROUPS - 4
            if n >= first_store:
                for m in range(0 if n == first_store else n, n + 1):
                    nc.sync.dma_start(out=o_view[m], in_=o_sb[:, m, :, :].rearrange("p u c -> p (u c)"))

        LAST = GROUPS - 1
        ALL = slice(0, U)
        transposes(0, (0, 1, 2, 3))
        new_codes(0)
        for u in range(U):
            quantise_tile(0, u)
        prepare_diagonal()
        transposes(1, (0, 1), spare_banks=True)
        transposes(1, (2, 3))
        plain_features(1, nc.scalar.copy)
        passes(0, 0)
        passes(0, 1)
        diag_passes(0)
        transposes(2, (0, 1))
        passes(0, 2)
        load_group(3)
        passes(0, 3)
        diag_transposes(0)
        transposes(2, (2, 3))
        plain_features(2, nc.scalar.copy)
        products(0, 0)
        products(0, 1)
        quantise(1)
        products(0, 2)
        products(0, 3)
        diag_product(0)
        quantise(2)
        first_adds(nc.gpsimd, 0, ALL)
        second_adds(nc.gpsimd, 0, slice(0, G_TILES))
        for n in range(1, LAST):
            more = n + 2 < GROUPS
            if n + 3 < GROUPS:
                load_group(n + 3)
            diag_passes(n)
            passes(n, 0)
            passes(n, 1)
            if more:
                transposes(n + 2, (0, 1))
            passes(n, 2)
            passes(n, 3)
            diag_transposes(n)
            if more:
                transposes(n + 2, (2, 3))
                plain_features(n + 2, nc.scalar.copy)
            for u in range(U):
                products(n, u)
            diag_product(n)
            if more:
                quantise(n + 2)
            first_adds(nc.gpsimd, n, ALL)
            second_adds(nc.gpsimd, n, slice(0, G_TILES))
            finish(n - 1, G_TILES)
        diag_passes(LAST)
        for u in range(U):
            passes(LAST, u)
        diag_transposes(LAST)
        products(LAST, 0)
        diag_product(LAST, slice(0, 1))
        adds(nc.gpsimd, LAST, slice(0, 1))
        for u in range(1, U):
            products(LAST, u)
        diag_product(LAST, slice(1, U))
        finish(LAST - 1, G_TILES)
        adds(nc.vector, LAST, slice(1, U))
        finish(LAST, U)
